import numpy as np
import ml_dtypes


def mxq(x, axis, fmt="e4m3"):
    dtype, down = {"e4m3": (ml_dtypes.float8_e4m3fn, 7), "e5m2": (ml_dtypes.float8_e5m2, 14)}[fmt]
    v = np.moveaxis(np.asarray(x, np.float32).astype(ml_dtypes.bfloat16).astype(np.float64), axis, -1)
    blocks = v.reshape(v.shape[:-1] + (-1, 32))
    amax = np.abs(blocks).max(-1, keepdims=True)
    byte = np.maximum(np.where(amax > 0, np.frexp(amax)[1] - 1 + 127, 0) - down, 1)
    scale = np.exp2(byte - 127.0)
    codes = (blocks / scale).astype(np.float32).astype(dtype).astype(np.float64)
    return np.moveaxis((codes * scale).reshape(v.shape), -1, axis)


WIDE = False


def mx_kscale(k):
    if not WIDE:
        return np.ones(k)
    levels = np.array([10, -10, 5, -5, 0])
    a = np.random.permutation(np.resize(levels, k // 512 * 4)).reshape(k // 512, 4)
    idx = np.arange(k)
    return np.exp2(a[idx // 512, idx % 128 // 32])


BF16 = ml_dtypes.bfloat16


def bf(x):
    return np.asarray(x, np.float32).astype(BF16)


def f64(x):
    return np.asarray(x).astype(np.float64)


E2M1 = np.array([0.0, 0.5, 1.0, 1.5, 2.0, 3.0, 4.0, 6.0, -0.0, -0.5, -1.0, -1.5, -2.0, -3.0, -4.0, -6.0])


def pack_weight(w, fmt):
    k, n = w.shape
    w = f64(bf(w)).reshape(k // 32, 32, n)
    amax = np.abs(w).max(1)
    if fmt == "e4m3":
        byte = np.frexp(amax)[1] - 1 + 127 - 7
    else:
        mant, ex = np.frexp(amax / 6.0)
        byte = np.where(mant > 0.5, ex, ex - 1) + 127
    byte = np.clip(np.where(amax > 0, byte, 1), 1, 254)
    scaled = (w * np.exp2(127.0 - byte)[:, None, :]).reshape(k, n).astype(np.float32)
    by_word = np.ascontiguousarray(scaled.reshape(k // 512, 128, 4, n).transpose(0, 1, 3, 2))
    if fmt == "e4m3":
        words = by_word.astype(ml_dtypes.float8_e4m3fn).view(np.uint8)
    else:
        c = by_word.astype(ml_dtypes.float4_e2m1fn).view(np.uint8) & 0xF
        words = c[..., 0::2] | (c[..., 1::2] << 4)
    return np.ascontiguousarray(words), np.ascontiguousarray(byte.astype(np.uint8).reshape(k // 512, 16, n))


def unpack_weight(words, scales, fmt):
    g, p, n, _ = words.shape
    if fmt == "e4m3":
        vals = np.ascontiguousarray(words).view(ml_dtypes.float8_e4m3fn).astype(np.float64)
    else:
        nib = np.empty((g, p, n, 4), np.uint8)
        nib[..., 0::2] = words & 0xF
        nib[..., 1::2] = words >> 4
        vals = E2M1[nib]
    vals = vals * np.repeat(np.exp2(scales.astype(np.float64) - 127.0), 8, axis=1)[..., None]
    return vals.transpose(0, 1, 3, 2).reshape(g * 512, n)


B, L, D, H, DK = 4, 256, 1024, 16, 64
E = H * DK
FMT = "e4m3"


def tropical_linear(t, w):
    return np.stack([np.max(t[n][:, None, :] + w[None, :, :], axis=-1) for n in range(t.shape[0])])


def split_heads(t):
    return t.reshape(B, L, H, DK).transpose(0, 2, 1, 3).reshape(B * H, L, DK)


def proj(xq, words, scales, lam):
    return np.log1p(np.maximum(xq @ unpack_weight(words, scales, FMT), 0.0)) - lam


def setup_inputs():
    s = mx_kscale(D)
    x = bf(np.random.standard_normal((B, L, D)) * s)
    Wq_words, Wq_scales = pack_weight(np.ascontiguousarray((np.random.standard_normal((E, D)) / np.sqrt(D) / s[None, :]).T), FMT)
    Wk_words, Wk_scales = pack_weight(np.ascontiguousarray((np.random.standard_normal((E, D)) / np.sqrt(D) / s[None, :]).T), FMT)
    Wv_words, Wv_scales = pack_weight(np.ascontiguousarray((np.random.standard_normal((E, D)) / np.sqrt(D) / s[None, :]).T), FMT)
    return {"x": x,
            "Wq_words": Wq_words, "Wq_scales": Wq_scales,
            "Wk_words": Wk_words, "Wk_scales": Wk_scales,
            "Wv_words": Wv_words, "Wv_scales": Wv_scales,
            "lam": bf(1.0 + 0.1 * np.random.standard_normal((1, 1, E))),
            "Wq_trop": bf(np.random.standard_normal((DK, DK))),
            "Wk_trop": bf(np.random.standard_normal((DK, DK))),
            "Wv_trop": bf(np.random.standard_normal((DK, DK)))}


def reference(x, Wq_words, Wq_scales, Wk_words, Wk_scales, Wv_words, Wv_scales, lam, Wq_trop, Wk_trop, Wv_trop):
    xq = mxq(f64(x), 2, "e4m3")
    lam = f64(lam)
    q = tropical_linear(split_heads(proj(xq, Wq_words, Wq_scales, lam)), f64(Wq_trop))
    k = tropical_linear(split_heads(proj(xq, Wk_words, Wk_scales, lam)), f64(Wk_trop))
    v = tropical_linear(split_heads(proj(xq, Wv_words, Wv_scales, lam)), f64(Wv_trop))
    return q, k, v

@@ -1,0 +1,200 @@
+from contextlib import ExitStack
+
+import concourse.masks as masks
+import concourse.mybir as mybir
+
+F32 = mybir.dt.float32
+BF16 = mybir.dt.bfloat16
+I32 = mybir.dt.int32
+U32 = mybir.dt.uint32
+U8 = mybir.dt.uint8
+FP8X4 = mybir.dt.float8_e4m3fn_x4
+ACT = mybir.ActivationFunctionType
+ALU = mybir.AluOpType
+
+P = 128
+BATCH, SEQ, D_IN, HEADS, DK = 4, 256, 1024, 16, 64
+ROWS = BATCH * SEQ
+FEATURES = HEADS * DK
+PACK = 4
+K_PASS = P * PACK
+PASSES = D_IN // K_PASS
+ROW_TILES = ROWS // P
+N_MOVING = 512
+ROW_HALVES = ROWS // N_MOVING
+TILES_PER_BANK = N_MOVING // P
+HEADS_PER_BLOCK = P // DK
+BLOCKS = FEATURES // P
+QUADRANTS = 4
+
+FLOPS = 3 * (2 * ROWS * D_IN * FEATURES + 2 * ROWS * HEADS * DK * DK)
+
+
+def tile_tropicalattention_pa_kernel(
+    tc,
+    x,
+    Wq_words,
+    Wq_scales,
+    Wk_words,
+    Wk_scales,
+    Wv_words,
+    Wv_scales,
+    lam,
+    Wq_trop,
+    Wk_trop,
+    Wv_trop,
+    out_0,
+    out_1,
+    out_2,
+):
+    nc = tc.nc
+    weights = [(Wq_words, Wq_scales), (Wk_words, Wk_scales), (Wv_words, Wv_scales)]
+    tropical = [Wq_trop, Wk_trop, Wv_trop]
+    outs = [out_0, out_1, out_2]
+    n_proj = len(outs)
+
+    with ExitStack() as ctx:
+        keep = ctx.enter_context(tc.tile_pool(name="keep", bufs=1))
+        setup = ctx.enter_context(tc.tile_pool(name="setup", bufs=2))
+        logs = ctx.enter_context(tc.tile_pool(name="logs", bufs=3))
+        relus = ctx.enter_context(tc.tile_pool(name="relus", bufs=2))
+        cands = ctx.enter_context(tc.tile_pool(name="cands", bufs=6))
+        results = ctx.enter_context(tc.tile_pool(name="results", bufs=3))
+        psum_mx = ctx.enter_context(tc.psum_pool(name="psum_mx", bufs=2))
+        psum_tr = ctx.enter_context(tc.psum_pool(name="psum_tr", bufs=6))
+
+        ident = keep.tile([P, P], F32, name="ident")
+        masks.make_identity(nc, ident[:])
+
+        x_rows = x.flatten_outer_dims()
+        x_sb = keep.tile([P, ROW_TILES, D_IN], BF16, name="x_sb")
+        for rt in range(ROW_TILES):
+            nc.sync.dma_start(out=x_sb[:, rt, :], in_=x_rows[rt * P : (rt + 1) * P, :])
+
+        w_codes = keep.tile([P, n_proj, PASSES, FEATURES], U32, name="w_codes", align_bytes=64)
+        w_scales = keep.tile([P, n_proj, PASSES, FEATURES], U8, name="w_scales", align_bytes=64)
+        nc.vector.memset(w_scales[:].bitcast(I32), 0)
+        for j, (words, scales) in enumerate(weights):
+            for g in range(PASSES):
+                nc.sync.dma_start(
+                    out=w_codes[:, j, g, :].bitcast(I32),
+                    in_=words[g].rearrange("p n t -> p (n t)").bitcast(I32),
+                )
+            scale_words = scales.bitcast(I32)
+            for quad in range(QUADRANTS):
+                nc.sync.dma_start(
+                    out=w_scales[32 * quad : 32 * quad + 4, j, :, :].bitcast(I32),
+                    in_=scale_words[:, 4 * quad : 4 * quad + 4, :].rearrange("g q n -> q g n"),
+                )
+
+        x_grouped = keep.tile([P, PASSES, ROWS * PACK], BF16, name="x_grouped", align_bytes=64)
+        x_codes = keep.tile([P, PASSES, ROWS], U32, name="x_codes", align_bytes=64)
+        x_scales = keep.tile([P, PASSES, ROWS], U8, name="x_scales", align_bytes=64)
+        for rt in range(ROW_TILES):
+            x_words = x_sb[:, rt, :].bitcast(F32)
+            xt = psum_tr.tile([P, PASSES, 2, P], F32, name="xt", tag="bank")
+            for g in range(PASSES):
+                for u in range(2):
+                    nc.tensor.transpose(
+                        xt[:, g, u, :],
+                        x_words[:, 256 * g + u : 256 * (g + 1) : 2],
+                        ident[:],
+                    )
+            nc.vector.tensor_copy(
+                out=x_grouped[:, :, rt * P * PACK : (rt + 1) * P * PACK]
+                .bitcast(F32)
+                .rearrange("p g (r u) -> p g r u", u=2),
+                in_=xt[:].rearrange("p g u r -> p g r u"),
+            )
+        for half in range(ROW_HALVES):
+            rows = slice(half * N_MOVING, (half + 1) * N_MOVING)
+            for g in range(PASSES):
+                nc.vector.quantize_mx(
+                    out=x_codes[:, g, rows].bitcast(FP8X4),
+                    scales=x_scales[:, g, rows],
+                    in_=x_grouped[:, g, half * N_MOVING * PACK : (half + 1) * N_MOVING * PACK],
+                )
+
+        lam_bf = setup.tile([BLOCKS, P], BF16, name="lam_bf")
+        nc.scalar.dma_start(out=lam_bf[:], in_=lam.rearrange("a b (f p) -> (a b f) p", p=P))
+        lam_sq = setup.tile([P, P], F32, name="lam_sq")
+        nc.vector.memset(lam_sq[:], 0.0)
+        nc.vector.tensor_copy(out=lam_sq[0:BLOCKS, :], in_=lam_bf[:])
+        lam_ps = psum_tr.tile([P, P], F32, name="lam_ps", tag="bank")
+        nc.tensor.transpose(lam_ps[:], lam_sq[:], ident[:])
+        lam_t = keep.tile([P, BLOCKS], F32, name="lam_t")
+        nc.vector.tensor_copy(out=lam_t[:], in_=lam_ps[:, 0:BLOCKS])
+
+        offsets = []
+        for j in range(n_proj):
+            t_bf = setup.tile([DK, DK], BF16, name="t_bf")
+            nc.scalar.dma_start(out=t_bf[:], in_=tropical[j])
+            t_sq = setup.tile([P, HEADS_PER_BLOCK, DK], F32, name="t_sq")
+            nc.vector.memset(t_sq[:], 0.0)
+            for h in range(HEADS_PER_BLOCK):
+                nc.vector.tensor_copy(out=t_sq[0:DK, h, :], in_=t_bf[:])
+            t_ps = psum_tr.tile([P, P], F32, name="t_ps", tag="bank")
+            nc.tensor.transpose(t_ps[:], t_sq[:].rearrange("p h i -> p (h i)"), ident[:])
+            offset = keep.tile([P, BLOCKS, DK], F32, name="offset%d" % j)
+            nc.vector.tensor_tensor(
+                out=offset[:],
+                in0=t_ps[:, 0:DK].unsqueeze(1).to_broadcast([P, BLOCKS, DK]),
+                in1=lam_t[:].unsqueeze(2).to_broadcast([P, BLOCKS, DK]),
+                op=ALU.subtract,
+            )
+            offsets.append(offset)
+
+        for j in range(n_proj):
+            for f in range(BLOCKS):
+                cols = slice(f * P, (f + 1) * P)
+                logp = logs.tile([P, ROWS], F32, name="logp")
+                for half in range(ROW_HALVES):
+                    rows = slice(half * N_MOVING, (half + 1) * N_MOVING)
+                    acc = psum_mx.tile([P, N_MOVING], F32, name="acc")
+                    for g in range(PASSES):
+                        nc.tensor.matmul_mx(
+                            out=acc[:],
+                            lhsT=w_codes[:, j, g, cols].bitcast(FP8X4),
+                            lhsT_scale=w_scales[:, j, g, cols],
+                            rhs=x_codes[:, g, rows].bitcast(FP8X4),
+                            rhs_scale=x_scales[:, g, rows],
+                            start=(g == 0),
+                            stop=(g == PASSES - 1),
+                        )
+                    relu = relus.tile([P, N_MOVING], F32, name="relu")
+                    nc.scalar.activation(out=relu[:], in_=acc[:], func=ACT.Relu)
+                    nc.scalar.activation(out=logp[:, rows], in_=relu[:], func=ACT.Ln, bias=1.0)
+
+                y = results.tile([P, ROW_TILES, HEADS_PER_BLOCK, DK], F32, name="y")
+                for o in range(DK):
+                    cand = cands.tile([P, ROWS], F32, name="cand")
+                    shift = offsets[j][:, f, o : o + 1]
+                    if o % 2 == 0:
+                        nc.scalar.activation(out=cand[:], in_=logp[:], func=ACT.Identity, bias=shift)
+                    else:
+                        nc.gpsimd.tensor_scalar(
+                            out=cand[:], in0=logp[:], scalar1=shift, scalar2=1.0,
+                            op0=ALU.add, op1=ALU.mult,
+                        )
+                    for bank in range(ROW_TILES // TILES_PER_BANK):
+                        turned = psum_tr.tile([P, TILES_PER_BANK, P], F32, name="turned", tag="bank")
+                        for r in range(TILES_PER_BANK):
+                            rt = bank * TILES_PER_BANK + r
+                            nc.tensor.transpose(
+                                turned[:, r, :], cand[:, rt * P : (rt + 1) * P], ident[:]
+                            )
+                        nc.vector.tensor_reduce(
+                            out=y[:, bank * TILES_PER_BANK : (bank + 1) * TILES_PER_BANK, :, o],
+                            in_=turned[:].rearrange("p r (h i) -> p r h i", h=HEADS_PER_BLOCK),
+                            axis=mybir.AxisListType.X,
+                            op=ALU.max,
+                        )
+
+                for rt in range(ROW_TILES):
+                    b, t = divmod(rt, SEQ // P)
+                    first = b * HEADS + f * HEADS_PER_BLOCK
+                    nc.sync.dma_start(
+                        out=outs[j][first : first + HEADS_PER_BLOCK, t * P : (t + 1) * P, :]
+                        .rearrange("h l o -> l h o"),
+                        in_=y[:, rt, :, :],
+                    )

@@ -23,9 +23,13 @@ ROW_TILES = ROWS // P
 N_MOVING = 512
 ROW_HALVES = ROWS // N_MOVING
 TILES_PER_BANK = N_MOVING // P
-HEADS_PER_BLOCK = P // DK
-BLOCKS = FEATURES // P
+SIDES = 2
+HALF = DK // SIDES
+HEADS_PER_BLOCK = P // HALF
+BLOCKS = HEADS // HEADS_PER_BLOCK
+CHUNKS = FEATURES // HALF // SIDES
 QUADRANTS = 4
+SPAN = 128.0
 
 FLOPS = 3 * (2 * ROWS * D_IN * FEATURES + 2 * ROWS * HEADS * DK * DK)
 
@@ -56,10 +60,10 @@ def tile_tropicalattention_pa_kernel(
     with ExitStack() as ctx:
         keep = ctx.enter_context(tc.tile_pool(name="keep", bufs=1))
         setup = ctx.enter_context(tc.tile_pool(name="setup", bufs=2))
-        logs = ctx.enter_context(tc.tile_pool(name="logs", bufs=3))
+        logs = ctx.enter_context(tc.tile_pool(name="logs", bufs=2))
         relus = ctx.enter_context(tc.tile_pool(name="relus", bufs=2))
-        cands = ctx.enter_context(tc.tile_pool(name="cands", bufs=6))
-        results = ctx.enter_context(tc.tile_pool(name="results", bufs=3))
+        cands = ctx.enter_context(tc.tile_pool(name="cands", bufs=4))
+        results = ctx.enter_context(tc.tile_pool(name="results", bufs=2))
         psum_mx = ctx.enter_context(tc.psum_pool(name="psum_mx", bufs=2))
         psum_tr = ctx.enter_context(tc.psum_pool(name="psum_tr", bufs=6))
 
@@ -71,20 +75,42 @@ def tile_tropicalattention_pa_kernel(
         for rt in range(ROW_TILES):
             nc.sync.dma_start(out=x_sb[:, rt, :], in_=x_rows[rt * P : (rt + 1) * P, :])
 
-        w_codes = keep.tile([P, n_proj, PASSES, FEATURES], U32, name="w_codes", align_bytes=64)
-        w_scales = keep.tile([P, n_proj, PASSES, FEATURES], U8, name="w_scales", align_bytes=64)
-        nc.vector.memset(w_scales[:].bitcast(I32), 0)
+        w_codes = keep.tile(
+            [P, n_proj, PASSES, SIDES, FEATURES // SIDES], U32, name="w_codes", align_bytes=64
+        )
+        raw_scales = keep.tile([P, n_proj, PASSES, FEATURES], U8, name="raw_scales")
+        w_scales = keep.tile(
+            [P, n_proj, PASSES, SIDES, FEATURES // SIDES], U8, name="w_scales", align_bytes=64
+        )
+        nc.vector.memset(raw_scales[:].bitcast(I32), 0)
         for j, (words, scales) in enumerate(weights):
             for g in range(PASSES):
-                nc.sync.dma_start(
-                    out=w_codes[:, j, g, :].bitcast(I32),
-                    in_=words[g].rearrange("p n t -> p (n t)").bitcast(I32),
+                by_side = (
+                    words[g]
+                    .rearrange("p n t -> p (n t)")
+                    .bitcast(I32)
+                    .rearrange("p (c s i) -> p c s i", s=SIDES, i=HALF)
                 )
+                for s in range(SIDES):
+                    nc.sync.dma_start(
+                        out=w_codes[:, j, g, s, :].bitcast(I32).rearrange("p (c i) -> p c i", i=HALF),
+                        in_=by_side[:, :, s, :],
+                    )
             scale_words = scales.bitcast(I32)
             for quad in range(QUADRANTS):
                 nc.sync.dma_start(
-                    out=w_scales[32 * quad : 32 * quad + 4, j, :, :].bitcast(I32),
+                    out=raw_scales[32 * quad : 32 * quad + 4, j, :, :].bitcast(I32),
                     in_=scale_words[:, 4 * quad : 4 * quad + 4, :].rearrange("g q n -> q g n"),
+                )
+            raw_by_side = (
+                raw_scales[:, j, :, :]
+                .bitcast(I32)
+                .rearrange("p g (c s w) -> p g c s w", s=SIDES, w=HALF // 4)
+            )
+            for s in range(SIDES):
+                nc.vector.tensor_copy(
+                    out=w_scales[:, j, :, s, :].bitcast(I32).rearrange("p g (c w) -> p g c w", w=HALF // 4),
+                    in_=raw_by_side[:, :, :, s, :],
                 )
 
         x_grouped = keep.tile([P, PASSES, ROWS * PACK], BF16, name="x_grouped", align_bytes=64)
@@ -115,77 +141,117 @@ def tile_tropicalattention_pa_kernel(
                     in_=x_grouped[:, g, half * N_MOVING * PACK : (half + 1) * N_MOVING * PACK],
                 )
 
-        lam_bf = setup.tile([BLOCKS, P], BF16, name="lam_bf")
-        nc.scalar.dma_start(out=lam_bf[:], in_=lam.rearrange("a b (f p) -> (a b f) p", p=P))
+        lam_bf = setup.tile([SIDES * BLOCKS, P], BF16, name="lam_bf")
+        lam_by_side = lam.rearrange("a b n -> (a b) n").rearrange(
+            "a (f h s i) -> a f h s i", h=HEADS_PER_BLOCK, s=SIDES, i=HALF
+        )
+        for s in range(SIDES):
+            nc.scalar.dma_start(
+                out=lam_bf[s * BLOCKS : (s + 1) * BLOCKS, :].rearrange("f (h i) -> f h i", i=HALF),
+                in_=lam_by_side[0, :, :, s, :],
+            )
         lam_sq = setup.tile([P, P], F32, name="lam_sq")
         nc.vector.memset(lam_sq[:], 0.0)
-        nc.vector.tensor_copy(out=lam_sq[0:BLOCKS, :], in_=lam_bf[:])
+        nc.vector.tensor_copy(out=lam_sq[0 : SIDES * BLOCKS, :], in_=lam_bf[:])
         lam_ps = psum_tr.tile([P, P], F32, name="lam_ps", tag="bank")
         nc.tensor.transpose(lam_ps[:], lam_sq[:], ident[:])
-        lam_t = keep.tile([P, BLOCKS], F32, name="lam_t")
-        nc.vector.tensor_copy(out=lam_t[:], in_=lam_ps[:, 0:BLOCKS])
+        lam_t = keep.tile([P, SIDES, BLOCKS], F32, name="lam_t")
+        nc.vector.tensor_copy(
+            out=lam_t[:].rearrange("p s f -> p (s f)"), in_=lam_ps[:, 0 : SIDES * BLOCKS]
+        )
 
-        offsets = []
+        bases = []
+        gaps = []
         for j in range(n_proj):
             t_bf = setup.tile([DK, DK], BF16, name="t_bf")
             nc.scalar.dma_start(out=t_bf[:], in_=tropical[j])
-            t_sq = setup.tile([P, HEADS_PER_BLOCK, DK], F32, name="t_sq")
+            t_sq = setup.tile([P, SIDES, HEADS_PER_BLOCK, HALF], F32, name="t_sq")
             nc.vector.memset(t_sq[:], 0.0)
-            for h in range(HEADS_PER_BLOCK):
-                nc.vector.tensor_copy(out=t_sq[0:DK, h, :], in_=t_bf[:])
-            t_ps = psum_tr.tile([P, P], F32, name="t_ps", tag="bank")
-            nc.tensor.transpose(t_ps[:], t_sq[:].rearrange("p h i -> p (h i)"), ident[:])
-            offset = keep.tile([P, BLOCKS, DK], F32, name="offset%d" % j)
-            nc.vector.tensor_tensor(
-                out=offset[:],
-                in0=t_ps[:, 0:DK].unsqueeze(1).to_broadcast([P, BLOCKS, DK]),
-                in1=lam_t[:].unsqueeze(2).to_broadcast([P, BLOCKS, DK]),
-                op=ALU.subtract,
+            t_ps = psum_tr.tile([P, SIDES, P], F32, name="t_ps", tag="bank")
+            shift = setup.tile([P, SIDES, BLOCKS, DK], F32, name="shift")
+            for s in range(SIDES):
+                nc.vector.tensor_copy(
+                    out=t_sq[0:DK, s, :, :],
+                    in_=t_bf[:, s * HALF : (s + 1) * HALF]
+                    .unsqueeze(1)
+                    .to_broadcast([DK, HEADS_PER_BLOCK, HALF]),
+                )
+                nc.tensor.transpose(
+                    t_ps[:, s, :], t_sq[:, s, :, :].rearrange("p h i -> p (h i)"), ident[:]
+                )
+                nc.vector.tensor_tensor(
+                    out=shift[:, s, :, :],
+                    in0=t_ps[:, s, 0:DK].unsqueeze(1).to_broadcast([P, BLOCKS, DK]),
+                    in1=lam_t[:, s, :].unsqueeze(2).to_broadcast([P, BLOCKS, DK]),
+                    op=ALU.subtract,
+                )
+            base = keep.tile([P, BLOCKS, DK], F32, name="base%d" % j)
+            nc.vector.scalar_tensor_tensor(
+                out=base[:], in0=shift[:, 1, :, :], scalar=-SPAN, in1=shift[:, 0, :, :],
+                op0=ALU.add, op1=ALU.max,
             )
-            offsets.append(offset)
+            other = setup.tile([P, BLOCKS, DK], F32, name="other")
+            nc.vector.scalar_tensor_tensor(
+                out=other[:], in0=shift[:, 0, :, :], scalar=-SPAN, in1=shift[:, 1, :, :],
+                op0=ALU.add, op1=ALU.max,
+            )
+            gap = keep.tile([P, BLOCKS, DK], F32, name="gap%d" % j)
+            nc.vector.tensor_tensor(out=gap[:], in0=other[:], in1=base[:], op=ALU.subtract)
+            bases.append(base)
+            gaps.append(gap)
 
         for j in range(n_proj):
             for f in range(BLOCKS):
                 cols = slice(f * P, (f + 1) * P)
-                logp = logs.tile([P, ROWS], F32, name="logp")
-                for half in range(ROW_HALVES):
-                    rows = slice(half * N_MOVING, (half + 1) * N_MOVING)
-                    acc = psum_mx.tile([P, N_MOVING], F32, name="acc")
-                    for g in range(PASSES):
-                        nc.tensor.matmul_mx(
-                            out=acc[:],
-                            lhsT=w_codes[:, j, g, cols].bitcast(FP8X4),
-                            lhsT_scale=w_scales[:, j, g, cols],
-                            rhs=x_codes[:, g, rows].bitcast(FP8X4),
-                            rhs_scale=x_scales[:, g, rows],
-                            start=(g == 0),
-                            stop=(g == PASSES - 1),
-                        )
-                    relu = relus.tile([P, N_MOVING], F32, name="relu")
-                    nc.scalar.activation(out=relu[:], in_=acc[:], func=ACT.Relu)
-                    nc.scalar.activation(out=logp[:, rows], in_=relu[:], func=ACT.Ln, bias=1.0)
+                logp = logs.tile([P, SIDES, ROWS], F32, name="logp")
+                for s in range(SIDES):
+                    for half in range(ROW_HALVES):
+                        rows = slice(half * N_MOVING, (half + 1) * N_MOVING)
+                        acc = psum_mx.tile([P, N_MOVING], F32, name="acc")
+                        for g in range(PASSES):
+                            nc.tensor.matmul_mx(
+                                out=acc[:],
+                                lhsT=w_codes[:, j, g, s, cols].bitcast(FP8X4),
+                                lhsT_scale=w_scales[:, j, g, s, cols],
+                                rhs=x_codes[:, g, rows].bitcast(FP8X4),
+                                rhs_scale=x_scales[:, g, rows],
+                                start=(g == 0),
+                                stop=(g == PASSES - 1),
+                            )
+                        relu = relus.tile([P, N_MOVING], F32, name="relu")
+                        nc.scalar.activation(out=relu[:], in_=acc[:], func=ACT.Relu)
+                        nc.scalar.activation(out=logp[:, s, rows], in_=relu[:], func=ACT.Ln, bias=1.0)
+                lead = logs.tile([P, ROWS], F32, name="lead")
+                nc.vector.tensor_tensor(
+                    out=lead[:], in0=logp[:, 1, :], in1=logp[:, 0, :], op=ALU.subtract
+                )
 
                 y = results.tile([P, ROW_TILES, HEADS_PER_BLOCK, DK], F32, name="y")
                 for o in range(DK):
-                    cand = cands.tile([P, ROWS], F32, name="cand")
-                    shift = offsets[j][:, f, o : o + 1]
-                    if o % 2 == 0:
-                        nc.scalar.activation(out=cand[:], in_=logp[:], func=ACT.Identity, bias=shift)
-                    else:
-                        nc.gpsimd.tensor_scalar(
-                            out=cand[:], in0=logp[:], scalar1=shift, scalar2=1.0,
-                            op0=ALU.add, op1=ALU.mult,
-                        )
+                    lower = cands.tile([P, ROWS], F32, name="lower")
+                    nc.gpsimd.tensor_scalar(
+                        out=lower[:], in0=logp[:, 0, :], scalar1=bases[j][:, f, o : o + 1],
+                        scalar2=1.0, op0=ALU.add, op1=ALU.mult,
+                    )
+                    excess = cands.tile([P, ROWS], F32, name="excess")
+                    nc.scalar.activation(
+                        out=excess[:], in_=lead[:], func=ACT.Relu, bias=gaps[j][:, f, o : o + 1]
+                    )
                     for bank in range(ROW_TILES // TILES_PER_BANK):
                         turned = psum_tr.tile([P, TILES_PER_BANK, P], F32, name="turned", tag="bank")
                         for r in range(TILES_PER_BANK):
                             rt = bank * TILES_PER_BANK + r
-                            nc.tensor.transpose(
-                                turned[:, r, :], cand[:, rt * P : (rt + 1) * P], ident[:]
+                            nc.tensor.matmul(
+                                out=turned[:, r, :], lhsT=lower[:, rt * P : (rt + 1) * P],
+                                rhs=ident[:], is_transpose=True, start=True, stop=False,
+                            )
+                            nc.tensor.matmul(
+                                out=turned[:, r, :], lhsT=excess[:, rt * P : (rt + 1) * P],
+                                rhs=ident[:], is_transpose=True, start=False, stop=True,
                             )
                         nc.vector.tensor_reduce(
                             out=y[:, bank * TILES_PER_BANK : (bank + 1) * TILES_PER_BANK, :, o],
-                            in_=turned[:].rearrange("p r (h i) -> p r h i", h=HEADS_PER_BLOCK),
+                            in_=turned[:].rearrange("p r (h i) -> p r h i", i=HALF),
                             axis=mybir.AxisListType.X,
                             op=ALU.max,
                         )

@@ -30,6 +30,7 @@ BLOCKS = HEADS // HEADS_PER_BLOCK
 CHUNKS = FEATURES // HALF // SIDES
 QUADRANTS = 4
 SPAN = 128.0
+AHEAD_AT = (16, 32, 48)
 
 FLOPS = 3 * (2 * ROWS * D_IN * FEATURES + 2 * ROWS * HEADS * DK * DK)
 
@@ -161,6 +162,7 @@ def tile_tropicalattention_pa_kernel(
         )
 
         bases = []
+        others = []
         gaps = []
         for j in range(n_proj):
             t_bf = setup.tile([DK, DK], BF16, name="t_bf")
@@ -190,7 +192,7 @@ def tile_tropicalattention_pa_kernel(
                 out=base[:], in0=shift[:, 1, :, :], scalar=-SPAN, in1=shift[:, 0, :, :],
                 op0=ALU.add, op1=ALU.max,
             )
-            other = setup.tile([P, BLOCKS, DK], F32, name="other")
+            other = keep.tile([P, BLOCKS, DK], F32, name="other%d" % j)
             nc.vector.scalar_tensor_tensor(
                 out=other[:], in0=shift[:, 0, :, :], scalar=-SPAN, in1=shift[:, 1, :, :],
                 op0=ALU.add, op1=ALU.max,
@@ -198,69 +200,90 @@ def tile_tropicalattention_pa_kernel(
             gap = keep.tile([P, BLOCKS, DK], F32, name="gap%d" % j)
             nc.vector.tensor_tensor(out=gap[:], in0=other[:], in1=base[:], op=ALU.subtract)
             bases.append(base)
+            others.append(other)
             gaps.append(gap)
 
-        for j in range(n_proj):
-            for f in range(BLOCKS):
-                cols = slice(f * P, (f + 1) * P)
-                logp = logs.tile([P, SIDES, ROWS], F32, name="logp")
-                for s in range(SIDES):
-                    for half in range(ROW_HALVES):
-                        rows = slice(half * N_MOVING, (half + 1) * N_MOVING)
-                        acc = psum_mx.tile([P, N_MOVING], F32, name="acc")
-                        for g in range(PASSES):
-                            nc.tensor.matmul_mx(
-                                out=acc[:],
-                                lhsT=w_codes[:, j, g, s, cols].bitcast(FP8X4),
-                                lhsT_scale=w_scales[:, j, g, s, cols],
-                                rhs=x_codes[:, g, rows].bitcast(FP8X4),
-                                rhs_scale=x_scales[:, g, rows],
-                                start=(g == 0),
-                                stop=(g == PASSES - 1),
-                            )
-                        relu = relus.tile([P, N_MOVING], F32, name="relu")
-                        nc.scalar.activation(out=relu[:], in_=acc[:], func=ACT.Relu)
-                        nc.scalar.activation(out=logp[:, s, rows], in_=relu[:], func=ACT.Ln, bias=1.0)
-                lead = logs.tile([P, ROWS], F32, name="lead")
-                nc.vector.tensor_tensor(
-                    out=lead[:], in0=logp[:, 1, :], in1=logp[:, 0, :], op=ALU.subtract
+        def side_logs(j, f, logp, s):
+            cols = slice(f * P, (f + 1) * P)
+            for half in range(ROW_HALVES):
+                rows = slice(half * N_MOVING, (half + 1) * N_MOVING)
+                acc = psum_mx.tile([P, N_MOVING], F32, name="acc")
+                for g in range(PASSES):
+                    nc.tensor.matmul_mx(
+                        out=acc[:],
+                        lhsT=w_codes[:, j, g, s, cols].bitcast(FP8X4),
+                        lhsT_scale=w_scales[:, j, g, s, cols],
+                        rhs=x_codes[:, g, rows].bitcast(FP8X4),
+                        rhs_scale=x_scales[:, g, rows],
+                        start=(g == 0),
+                        stop=(g == PASSES - 1),
+                    )
+                relu = relus.tile([P, N_MOVING], F32, name="relu")
+                nc.scalar.activation(out=relu[:], in_=acc[:], func=ACT.Relu)
+                nc.scalar.activation(out=logp[:, s, rows], in_=relu[:], func=ACT.Ln, bias=1.0)
+
+        def side_difference(logp, lead):
+            nc.vector.tensor_tensor(
+                out=lead[:], in0=logp[:, 1, :], in1=logp[:, 0, :], op=ALU.subtract
+            )
+
+        blocks = [(j, f) for j in range(n_proj) for f in range(BLOCKS)]
+        logp = logs.tile([P, SIDES, ROWS], F32, name="logp")
+        lead = logs.tile([P, ROWS], F32, name="lead")
+        for s in range(SIDES):
+            side_logs(blocks[0][0], blocks[0][1], logp, s)
+        side_difference(logp, lead)
+
+        for index, (j, f) in enumerate(blocks):
+            following = blocks[index + 1] if index + 1 < len(blocks) else None
+            next_logp = None
+            next_lead = None
+            y = results.tile([P, ROW_TILES, HEADS_PER_BLOCK, DK], F32, name="y")
+            for o in range(DK):
+                if following is not None:
+                    if o == AHEAD_AT[0]:
+                        next_logp = logs.tile([P, SIDES, ROWS], F32, name="logp")
+                        next_lead = logs.tile([P, ROWS], F32, name="lead")
+                        side_logs(following[0], following[1], next_logp, 0)
+                    elif o == AHEAD_AT[1]:
+                        side_logs(following[0], following[1], next_logp, 1)
+                    elif o == AHEAD_AT[2]:
+                        side_difference(next_logp, next_lead)
+                lower = cands.tile([P, ROWS], F32, name="lower")
+                nc.gpsimd.tensor_scalar(
+                    out=lower[:], in0=logp[:, 0, :], scalar1=bases[j][:, f, o : o + 1],
+                    scalar2=1.0, op0=ALU.add, op1=ALU.mult,
                 )
-
-                y = results.tile([P, ROW_TILES, HEADS_PER_BLOCK, DK], F32, name="y")
-                for o in range(DK):
-                    lower = cands.tile([P, ROWS], F32, name="lower")
-                    nc.gpsimd.tensor_scalar(
-                        out=lower[:], in0=logp[:, 0, :], scalar1=bases[j][:, f, o : o + 1],
-                        scalar2=1.0, op0=ALU.add, op1=ALU.mult,
-                    )
-                    excess = cands.tile([P, ROWS], F32, name="excess")
-                    nc.scalar.activation(
-                        out=excess[:], in_=lead[:], func=ACT.Relu, bias=gaps[j][:, f, o : o + 1]
-                    )
-                    for bank in range(ROW_TILES // TILES_PER_BANK):
-                        turned = psum_tr.tile([P, TILES_PER_BANK, P], F32, name="turned", tag="bank")
-                        for r in range(TILES_PER_BANK):
-                            rt = bank * TILES_PER_BANK + r
-                            nc.tensor.matmul(
-                                out=turned[:, r, :], lhsT=lower[:, rt * P : (rt + 1) * P],
-                                rhs=ident[:], is_transpose=True, start=True, stop=False,
-                            )
-                            nc.tensor.matmul(
-                                out=turned[:, r, :], lhsT=excess[:, rt * P : (rt + 1) * P],
-                                rhs=ident[:], is_transpose=True, start=False, stop=True,
-                            )
-                        nc.vector.tensor_reduce(
-                            out=y[:, bank * TILES_PER_BANK : (bank + 1) * TILES_PER_BANK, :, o],
-                            in_=turned[:].rearrange("p r (h i) -> p r h i", i=HALF),
-                            axis=mybir.AxisListType.X,
-                            op=ALU.max,
+                excess = cands.tile([P, ROWS], F32, name="excess")
+                nc.scalar.activation(
+                    out=excess[:], in_=lead[:], func=ACT.Relu, bias=gaps[j][:, f, o : o + 1]
+                )
+                first, second = lower[:], excess[:]
+                for bank in range(ROW_TILES // TILES_PER_BANK):
+                    turned = psum_tr.tile([P, TILES_PER_BANK, P], F32, name="turned", tag="bank")
+                    for r in range(TILES_PER_BANK):
+                        rt = bank * TILES_PER_BANK + r
+                        nc.tensor.matmul(
+                            out=turned[:, r, :], lhsT=first[:, rt * P : (rt + 1) * P],
+                            rhs=ident[:], is_transpose=True, start=True, stop=False,
                         )
-
-                for rt in range(ROW_TILES):
-                    b, t = divmod(rt, SEQ // P)
-                    first = b * HEADS + f * HEADS_PER_BLOCK
-                    nc.sync.dma_start(
-                        out=outs[j][first : first + HEADS_PER_BLOCK, t * P : (t + 1) * P, :]
-                        .rearrange("h l o -> l h o"),
-                        in_=y[:, rt, :, :],
+                        nc.tensor.matmul(
+                            out=turned[:, r, :], lhsT=second[:, rt * P : (rt + 1) * P],
+                            rhs=ident[:], is_transpose=True, start=False, stop=True,
+                        )
+                    nc.vector.tensor_reduce(
+                        out=y[:, bank * TILES_PER_BANK : (bank + 1) * TILES_PER_BANK, :, o],
+                        in_=turned[:].rearrange("p r (h i) -> p r h i", i=HALF),
+                        axis=mybir.AxisListType.X,
+                        op=ALU.max,
                     )
+
+            for rt in range(ROW_TILES):
+                b, t = divmod(rt, SEQ // P)
+                first_head = b * HEADS + f * HEADS_PER_BLOCK
+                nc.sync.dma_start(
+                    out=outs[j][first_head : first_head + HEADS_PER_BLOCK, t * P : (t + 1) * P, :]
+                    .rearrange("h l o -> l h o"),
+                    in_=y[:, rt, :, :],
+                )
+            logp, lead = next_logp, next_lead

@@ -31,6 +31,9 @@ CHUNKS = FEATURES // HALF // SIDES
 QUADRANTS = 4
 SPAN = 128.0
 AHEAD_AT = (16, 32, 48)
+PAIR_ON_VECTOR = tuple(range(3, 60, 7))
+PREPARE_AHEAD = 2
+REFILL_AT = 61
 
 FLOPS = 3 * (2 * ROWS * D_IN * FEATURES + 2 * ROWS * HEADS * DK * DK)
 
@@ -66,7 +69,9 @@ def tile_tropicalattention_pa_kernel(
         cands = ctx.enter_context(tc.tile_pool(name="cands", bufs=4))
         results = ctx.enter_context(tc.tile_pool(name="results", bufs=2))
         psum_mx = ctx.enter_context(tc.psum_pool(name="psum_mx", bufs=2))
-        psum_tr = ctx.enter_context(tc.psum_pool(name="psum_tr", bufs=6))
+        psum_tr = ctx.enter_context(tc.psum_pool(name="psum_tr", bufs=4))
+        psum_keep = ctx.enter_context(tc.psum_pool(name="psum_keep", bufs=1))
+        pairs = ctx.enter_context(tc.tile_pool(name="pairs", bufs=2))
 
         ident = keep.tile([P, P], F32, name="ident")
         masks.make_identity(nc, ident[:])
@@ -227,17 +232,53 @@ def tile_tropicalattention_pa_kernel(
                 out=lead[:], in0=logp[:, 1, :], in1=logp[:, 0, :], op=ALU.subtract
             )
 
+        def side1_into_psum(logp):
+            rows_first = pairs.tile([P, ROW_TILES, P], F32, name="rows_first")
+            for bank in range(ROW_HALVES):
+                turned = psum_tr.tile([P, TILES_PER_BANK, P], F32, name="turned", tag="bank")
+                for r in range(TILES_PER_BANK):
+                    rt = bank * TILES_PER_BANK + r
+                    nc.tensor.transpose(turned[:, r, :], logp[:, 1, rt * P : (rt + 1) * P], ident[:])
+                nc.scalar.copy(
+                    out=rows_first[:, bank * TILES_PER_BANK : (bank + 1) * TILES_PER_BANK, :], in_=turned[:]
+                )
+            halves = []
+            for bank in range(ROW_HALVES):
+                back = psum_keep.tile([P, TILES_PER_BANK, P], F32, name="back%d" % bank)
+                for r in range(TILES_PER_BANK):
+                    nc.tensor.transpose(back[:, r, :], rows_first[:, bank * TILES_PER_BANK + r, :], ident[:])
+                halves.append(back)
+            return halves
+
+        def better_side(j, f, o, logp, log1_psum):
+            lower = pairs.tile([P, ROWS], F32, name="pair_lower")
+            nc.scalar.activation(
+                out=lower[:], in_=logp[:, 0, :], func=ACT.Identity, bias=bases[j][:, f, o : o + 1]
+            )
+            better = pairs.tile([P, ROWS], F32, name="pair_better")
+            for bank in range(ROW_HALVES):
+                rows = slice(bank * N_MOVING, (bank + 1) * N_MOVING)
+                nc.vector.scalar_tensor_tensor(
+                    out=better[:, rows], in0=log1_psum[bank][:].rearrange("p r c -> p (r c)"),
+                    scalar=others[j][:, f, o : o + 1], in1=lower[:, rows],
+                    op0=ALU.add, op1=ALU.max,
+                )
+            return better
+
         blocks = [(j, f) for j in range(n_proj) for f in range(BLOCKS)]
         logp = logs.tile([P, SIDES, ROWS], F32, name="logp")
         lead = logs.tile([P, ROWS], F32, name="lead")
         for s in range(SIDES):
             side_logs(blocks[0][0], blocks[0][1], logp, s)
         side_difference(logp, lead)
+        log1_psum = side1_into_psum(logp)
 
         for index, (j, f) in enumerate(blocks):
             following = blocks[index + 1] if index + 1 < len(blocks) else None
             next_logp = None
             next_lead = None
+            next_log1_psum = None
+            prepared = {}
             y = results.tile([P, ROW_TILES, HEADS_PER_BLOCK, DK], F32, name="y")
             for o in range(DK):
                 if following is not None:
@@ -249,28 +290,33 @@ def tile_tropicalattention_pa_kernel(
                         side_logs(following[0], following[1], next_logp, 1)
                     elif o == AHEAD_AT[2]:
                         side_difference(next_logp, next_lead)
-                lower = cands.tile([P, ROWS], F32, name="lower")
-                nc.gpsimd.tensor_scalar(
-                    out=lower[:], in0=logp[:, 0, :], scalar1=bases[j][:, f, o : o + 1],
-                    scalar2=1.0, op0=ALU.add, op1=ALU.mult,
-                )
-                excess = cands.tile([P, ROWS], F32, name="excess")
-                nc.scalar.activation(
-                    out=excess[:], in_=lead[:], func=ACT.Relu, bias=gaps[j][:, f, o : o + 1]
-                )
-                first, second = lower[:], excess[:]
+                    elif o == REFILL_AT:
+                        next_log1_psum = side1_into_psum(next_logp)
+                if o + PREPARE_AHEAD in PAIR_ON_VECTOR:
+                    prepared[o + PREPARE_AHEAD] = better_side(j, f, o + PREPARE_AHEAD, logp, log1_psum)
+                if o in PAIR_ON_VECTOR:
+                    terms = [prepared[o][:]]
+                else:
+                    lower = cands.tile([P, ROWS], F32, name="lower")
+                    nc.gpsimd.tensor_scalar(
+                        out=lower[:], in0=logp[:, 0, :], scalar1=bases[j][:, f, o : o + 1],
+                        scalar2=1.0, op0=ALU.add, op1=ALU.mult,
+                    )
+                    excess = cands.tile([P, ROWS], F32, name="excess")
+                    nc.scalar.activation(
+                        out=excess[:], in_=lead[:], func=ACT.Relu, bias=gaps[j][:, f, o : o + 1]
+                    )
+                    terms = [lower[:], excess[:]]
                 for bank in range(ROW_TILES // TILES_PER_BANK):
                     turned = psum_tr.tile([P, TILES_PER_BANK, P], F32, name="turned", tag="bank")
                     for r in range(TILES_PER_BANK):
                         rt = bank * TILES_PER_BANK + r
-                        nc.tensor.matmul(
-                            out=turned[:, r, :], lhsT=first[:, rt * P : (rt + 1) * P],
-                            rhs=ident[:], is_transpose=True, start=True, stop=False,
-                        )
-                        nc.tensor.matmul(
-                            out=turned[:, r, :], lhsT=second[:, rt * P : (rt + 1) * P],
-                            rhs=ident[:], is_transpose=True, start=False, stop=True,
-                        )
+                        for number, term in enumerate(terms):
+                            nc.tensor.matmul(
+                                out=turned[:, r, :], lhsT=term[:, rt * P : (rt + 1) * P],
+                                rhs=ident[:], is_transpose=True,
+                                start=(number == 0), stop=(number == len(terms) - 1),
+                            )
                     nc.vector.tensor_reduce(
                         out=y[:, bank * TILES_PER_BANK : (bank + 1) * TILES_PER_BANK, :, o],
                         in_=turned[:].rearrange("p r (h i) -> p r h i", i=HALF),
@@ -286,4 +332,4 @@ def tile_tropicalattention_pa_kernel(
                     .rearrange("h l o -> l h o"),
                     in_=y[:, rt, :, :],
                 )
-            logp, lead = next_logp, next_lead
+            logp, lead, log1_psum = next_logp, next_lead, next_log1_psum

@@ -31,9 +31,10 @@ CHUNKS = FEATURES // HALF // SIDES
 QUADRANTS = 4
 SPAN = 128.0
 AHEAD_AT = (16, 32, 48)
-PAIR_ON_VECTOR = tuple(range(3, 60, 7))
-PREPARE_AHEAD = 2
-REFILL_AT = 61
+PAIR_ON_VECTOR = tuple(range(6, 63, 7))
+VECTOR_AHEAD = 9
+SCALAR_AHEAD = 2
+REFILL_AT = 55
 
 FLOPS = 3 * (2 * ROWS * D_IN * FEATURES + 2 * ROWS * HEADS * DK * DK)
 
@@ -68,8 +69,7 @@ def tile_tropicalattention_pa_kernel(
         relus = ctx.enter_context(tc.tile_pool(name="relus", bufs=2))
         cands = ctx.enter_context(tc.tile_pool(name="cands", bufs=4))
         results = ctx.enter_context(tc.tile_pool(name="results", bufs=2))
-        psum_mx = ctx.enter_context(tc.psum_pool(name="psum_mx", bufs=2))
-        psum_tr = ctx.enter_context(tc.psum_pool(name="psum_tr", bufs=4))
+        psum_tr = ctx.enter_context(tc.psum_pool(name="psum_tr", bufs=6))
         psum_keep = ctx.enter_context(tc.psum_pool(name="psum_keep", bufs=1))
         pairs = ctx.enter_context(tc.tile_pool(name="pairs", bufs=2))
 
@@ -212,7 +212,7 @@ def tile_tropicalattention_pa_kernel(
             cols = slice(f * P, (f + 1) * P)
             for half in range(ROW_HALVES):
                 rows = slice(half * N_MOVING, (half + 1) * N_MOVING)
-                acc = psum_mx.tile([P, N_MOVING], F32, name="acc")
+                acc = psum_tr.tile([P, N_MOVING], F32, name="acc", tag="bank")
                 for g in range(PASSES):
                     nc.tensor.matmul_mx(
                         out=acc[:],
@@ -250,22 +250,29 @@ def tile_tropicalattention_pa_kernel(
                 halves.append(back)
             return halves
 
-        def better_side(j, f, o, logp, log1_psum):
-            lower = pairs.tile([P, ROWS], F32, name="pair_lower")
-            nc.scalar.activation(
-                out=lower[:], in_=logp[:, 0, :], func=ACT.Identity, bias=bases[j][:, f, o : o + 1]
-            )
-            better = pairs.tile([P, ROWS], F32, name="pair_better")
+        def better_less_other(j, f, o, logp, log1_psum):
+            less = pairs.tile([P, ROWS], F32, name="pair_less")
             for bank in range(ROW_HALVES):
                 rows = slice(bank * N_MOVING, (bank + 1) * N_MOVING)
                 nc.vector.scalar_tensor_tensor(
-                    out=better[:, rows], in0=log1_psum[bank][:].rearrange("p r c -> p (r c)"),
-                    scalar=others[j][:, f, o : o + 1], in1=lower[:, rows],
-                    op0=ALU.add, op1=ALU.max,
+                    out=less[:, rows], in0=logp[:, 0, rows],
+                    scalar=gaps[j][:, f, o : o + 1],
+                    in1=log1_psum[bank][:].rearrange("p r c -> p (r c)"),
+                    op0=ALU.subtract, op1=ALU.max,
                 )
+            return less
+
+        def add_other(j, f, o, less):
+            better = pairs.tile([P, ROWS], F32, name="pair_better")
+            nc.scalar.activation(
+                out=better[:], in_=less[:], func=ACT.Identity, bias=others[j][:, f, o : o + 1]
+            )
             return better
 
         blocks = [(j, f) for j in range(n_proj) for f in range(BLOCKS)]
+        vector_at = {}
+        for pair_step in PAIR_ON_VECTOR:
+            vector_at[max(0, pair_step - VECTOR_AHEAD)] = pair_step
         logp = logs.tile([P, SIDES, ROWS], F32, name="logp")
         lead = logs.tile([P, ROWS], F32, name="lead")
         for s in range(SIDES):
@@ -279,6 +286,7 @@ def tile_tropicalattention_pa_kernel(
             next_lead = None
             next_log1_psum = None
             prepared = {}
+            halfway = {}
             y = results.tile([P, ROW_TILES, HEADS_PER_BLOCK, DK], F32, name="y")
             for o in range(DK):
                 if following is not None:
@@ -292,8 +300,10 @@ def tile_tropicalattention_pa_kernel(
                         side_difference(next_logp, next_lead)
                     elif o == REFILL_AT:
                         next_log1_psum = side1_into_psum(next_logp)
-                if o + PREPARE_AHEAD in PAIR_ON_VECTOR:
-                    prepared[o + PREPARE_AHEAD] = better_side(j, f, o + PREPARE_AHEAD, logp, log1_psum)
+                if o in vector_at:
+                    halfway[vector_at[o]] = better_less_other(j, f, vector_at[o], logp, log1_psum)
+                if o + SCALAR_AHEAD in PAIR_ON_VECTOR:
+                    prepared[o + SCALAR_AHEAD] = add_other(j, f, o + SCALAR_AHEAD, halfway[o + SCALAR_AHEAD])
                 if o in PAIR_ON_VECTOR:
                     terms = [prepared[o][:]]
                 else:

@@ -31,7 +31,8 @@ CHUNKS = FEATURES // HALF // SIDES
 QUADRANTS = 4
 SPAN = 128.0
 AHEAD_AT = (16, 32, 48)
-PAIR_ON_VECTOR = tuple(range(6, 63, 7))
+LATER_AT = (6, 12)
+PAIR_ON_VECTOR = tuple(range(8, 63, 9))
 VECTOR_AHEAD = 9
 SCALAR_AHEAD = 2
 REFILL_AT = 55
@@ -78,36 +79,45 @@ def tile_tropicalattention_pa_kernel(
 
         x_rows = x.flatten_outer_dims()
         x_sb = keep.tile([P, ROW_TILES, D_IN], BF16, name="x_sb")
-        for rt in range(ROW_TILES):
+
+        def load_x(rt):
             nc.sync.dma_start(out=x_sb[:, rt, :], in_=x_rows[rt * P : (rt + 1) * P, :])
 
         w_codes = keep.tile(
             [P, n_proj, PASSES, SIDES, FEATURES // SIDES], U32, name="w_codes", align_bytes=64
         )
-        raw_scales = keep.tile([P, n_proj, PASSES, FEATURES], U8, name="raw_scales")
-        w_scales = keep.tile(
-            [P, n_proj, PASSES, SIDES, FEATURES // SIDES], U8, name="w_scales", align_bytes=64
-        )
-        nc.vector.memset(raw_scales[:].bitcast(I32), 0)
-        for j, (words, scales) in enumerate(weights):
+
+        def load_codes(j, first_head, last_head):
             for g in range(PASSES):
                 by_side = (
-                    words[g]
+                    weights[j][0][g]
                     .rearrange("p n t -> p (n t)")
                     .bitcast(I32)
                     .rearrange("p (c s i) -> p c s i", s=SIDES, i=HALF)
                 )
                 for s in range(SIDES):
                     nc.sync.dma_start(
-                        out=w_codes[:, j, g, s, :].bitcast(I32).rearrange("p (c i) -> p c i", i=HALF),
-                        in_=by_side[:, :, s, :],
+                        out=w_codes[:, j, g, s, first_head * HALF : last_head * HALF]
+                        .bitcast(I32)
+                        .rearrange("p (c i) -> p c i", i=HALF),
+                        in_=by_side[:, first_head:last_head, s, :],
                     )
-            scale_words = scales.bitcast(I32)
+
+        raw_scales = keep.tile([P, n_proj, PASSES, FEATURES], U8, name="raw_scales")
+        w_scales = keep.tile(
+            [P, n_proj, PASSES, SIDES, FEATURES // SIDES], U8, name="w_scales", align_bytes=64
+        )
+        nc.vector.memset(raw_scales[:].bitcast(I32), 0)
+
+        def load_scale_rows(j):
+            scale_words = weights[j][1].bitcast(I32)
             for quad in range(QUADRANTS):
                 nc.sync.dma_start(
                     out=raw_scales[32 * quad : 32 * quad + 4, j, :, :].bitcast(I32),
                     in_=scale_words[:, 4 * quad : 4 * quad + 4, :].rearrange("g q n -> q g n"),
                 )
+
+        def scales_side_first(j):
             raw_by_side = (
                 raw_scales[:, j, :, :]
                 .bitcast(I32)
@@ -119,34 +129,6 @@ def tile_tropicalattention_pa_kernel(
                     in_=raw_by_side[:, :, :, s, :],
                 )
 
-        x_grouped = keep.tile([P, PASSES, ROWS * PACK], BF16, name="x_grouped", align_bytes=64)
-        x_codes = keep.tile([P, PASSES, ROWS], U32, name="x_codes", align_bytes=64)
-        x_scales = keep.tile([P, PASSES, ROWS], U8, name="x_scales", align_bytes=64)
-        for rt in range(ROW_TILES):
-            x_words = x_sb[:, rt, :].bitcast(F32)
-            xt = psum_tr.tile([P, PASSES, 2, P], F32, name="xt", tag="bank")
-            for g in range(PASSES):
-                for u in range(2):
-                    nc.tensor.transpose(
-                        xt[:, g, u, :],
-                        x_words[:, 256 * g + u : 256 * (g + 1) : 2],
-                        ident[:],
-                    )
-            nc.vector.tensor_copy(
-                out=x_grouped[:, :, rt * P * PACK : (rt + 1) * P * PACK]
-                .bitcast(F32)
-                .rearrange("p g (r u) -> p g r u", u=2),
-                in_=xt[:].rearrange("p g u r -> p g r u"),
-            )
-        for half in range(ROW_HALVES):
-            rows = slice(half * N_MOVING, (half + 1) * N_MOVING)
-            for g in range(PASSES):
-                nc.vector.quantize_mx(
-                    out=x_codes[:, g, rows].bitcast(FP8X4),
-                    scales=x_scales[:, g, rows],
-                    in_=x_grouped[:, g, half * N_MOVING * PACK : (half + 1) * N_MOVING * PACK],
-                )
-
         lam_bf = setup.tile([SIDES * BLOCKS, P], BF16, name="lam_bf")
         lam_by_side = lam.rearrange("a b n -> (a b) n").rearrange(
             "a (f h s i) -> a f h s i", h=HEADS_PER_BLOCK, s=SIDES, i=HALF
@@ -156,6 +138,53 @@ def tile_tropicalattention_pa_kernel(
                 out=lam_bf[s * BLOCKS : (s + 1) * BLOCKS, :].rearrange("f (h i) -> f h i", i=HALF),
                 in_=lam_by_side[0, :, :, s, :],
             )
+        t_bfs = []
+        for j in range(n_proj):
+            t_bf = keep.tile([DK, DK], BF16, name="t_bf%d" % j)
+            nc.scalar.dma_start(out=t_bf[:], in_=tropical[j])
+            t_bfs.append(t_bf)
+        tiles_per_half = ROW_TILES // ROW_HALVES
+        for rt in range(tiles_per_half):
+            load_x(rt)
+        load_scale_rows(0)
+        load_codes(0, 0, HEADS_PER_BLOCK)
+        for rt in range(tiles_per_half, ROW_TILES):
+            load_x(rt)
+        load_codes(0, HEADS_PER_BLOCK, HEADS)
+        for j in range(1, n_proj):
+            load_scale_rows(j)
+            load_codes(j, 0, HEADS)
+
+        x_grouped = keep.tile([P, PASSES, ROWS * PACK], BF16, name="x_grouped", align_bytes=64)
+        x_codes = keep.tile([P, PASSES, ROWS], U32, name="x_codes", align_bytes=64)
+        x_scales = keep.tile([P, PASSES, ROWS], U8, name="x_scales", align_bytes=64)
+        for half in range(ROW_HALVES):
+            for rt in range(half * tiles_per_half, (half + 1) * tiles_per_half):
+                x_words = x_sb[:, rt, :].bitcast(F32)
+                xt = psum_tr.tile([P, PASSES, 2, P], F32, name="xt", tag="bank")
+                for g in range(PASSES):
+                    for u in range(2):
+                        nc.tensor.transpose(
+                            xt[:, g, u, :],
+                            x_words[:, 256 * g + u : 256 * (g + 1) : 2],
+                            ident[:],
+                        )
+                nc.vector.tensor_copy(
+                    out=x_grouped[:, :, rt * P * PACK : (rt + 1) * P * PACK]
+                    .bitcast(F32)
+                    .rearrange("p g (r u) -> p g r u", u=2),
+                    in_=xt[:].rearrange("p g u r -> p g r u"),
+                )
+            rows = slice(half * N_MOVING, (half + 1) * N_MOVING)
+            for g in range(PASSES):
+                nc.vector.quantize_mx(
+                    out=x_codes[:, g, rows].bitcast(FP8X4),
+                    scales=x_scales[:, g, rows],
+                    in_=x_grouped[:, g, half * N_MOVING * PACK : (half + 1) * N_MOVING * PACK],
+                )
+            if half == 0:
+                scales_side_first(0)
+
         lam_sq = setup.tile([P, P], F32, name="lam_sq")
         nc.vector.memset(lam_sq[:], 0.0)
         nc.vector.tensor_copy(out=lam_sq[0 : SIDES * BLOCKS, :], in_=lam_bf[:])
@@ -166,12 +195,7 @@ def tile_tropicalattention_pa_kernel(
             out=lam_t[:].rearrange("p s f -> p (s f)"), in_=lam_ps[:, 0 : SIDES * BLOCKS]
         )
 
-        bases = []
-        others = []
-        gaps = []
-        for j in range(n_proj):
-            t_bf = setup.tile([DK, DK], BF16, name="t_bf")
-            nc.scalar.dma_start(out=t_bf[:], in_=tropical[j])
+        def shifts(j):
             t_sq = setup.tile([P, SIDES, HEADS_PER_BLOCK, HALF], F32, name="t_sq")
             nc.vector.memset(t_sq[:], 0.0)
             t_ps = psum_tr.tile([P, SIDES, P], F32, name="t_ps", tag="bank")
@@ -179,7 +203,7 @@ def tile_tropicalattention_pa_kernel(
             for s in range(SIDES):
                 nc.vector.tensor_copy(
                     out=t_sq[0:DK, s, :, :],
-                    in_=t_bf[:, s * HALF : (s + 1) * HALF]
+                    in_=t_bfs[j][:, s * HALF : (s + 1) * HALF]
                     .unsqueeze(1)
                     .to_broadcast([DK, HEADS_PER_BLOCK, HALF]),
                 )
@@ -192,6 +216,13 @@ def tile_tropicalattention_pa_kernel(
                     in1=lam_t[:, s, :].unsqueeze(2).to_broadcast([P, BLOCKS, DK]),
                     op=ALU.subtract,
                 )
+            return shift
+
+        bases = {}
+        others = {}
+        gaps = {}
+
+        def base_and_gap(j, shift):
             base = keep.tile([P, BLOCKS, DK], F32, name="base%d" % j)
             nc.vector.scalar_tensor_tensor(
                 out=base[:], in0=shift[:, 1, :, :], scalar=-SPAN, in1=shift[:, 0, :, :],
@@ -204,9 +235,11 @@ def tile_tropicalattention_pa_kernel(
             )
             gap = keep.tile([P, BLOCKS, DK], F32, name="gap%d" % j)
             nc.vector.tensor_tensor(out=gap[:], in0=other[:], in1=base[:], op=ALU.subtract)
-            bases.append(base)
-            others.append(other)
-            gaps.append(gap)
+            bases[j] = base
+            others[j] = other
+            gaps[j] = gap
+
+        base_and_gap(0, shifts(0))
 
         def side_logs(j, f, logp, s):
             cols = slice(f * P, (f + 1) * P)
@@ -228,7 +261,7 @@ def tile_tropicalattention_pa_kernel(
                 nc.scalar.activation(out=logp[:, s, rows], in_=relu[:], func=ACT.Ln, bias=1.0)
 
         def side_difference(logp, lead):
-            nc.vector.tensor_tensor(
+            nc.gpsimd.tensor_tensor(
                 out=lead[:], in0=logp[:, 1, :], in1=logp[:, 0, :], op=ALU.subtract
             )
 
@@ -279,6 +312,9 @@ def tile_tropicalattention_pa_kernel(
             side_logs(blocks[0][0], blocks[0][1], logp, s)
         side_difference(logp, lead)
         log1_psum = side1_into_psum(logp)
+        later_shifts = {}
+        for later in range(1, n_proj):
+            later_shifts[later] = shifts(later)
 
         for index, (j, f) in enumerate(blocks):
             following = blocks[index + 1] if index + 1 < len(blocks) else None
@@ -289,6 +325,10 @@ def tile_tropicalattention_pa_kernel(
             halfway = {}
             y = results.tile([P, ROW_TILES, HEADS_PER_BLOCK, DK], F32, name="y")
             for o in range(DK):
+                if index == 0 and o in LATER_AT:
+                    later = 1 + LATER_AT.index(o)
+                    scales_side_first(later)
+                    base_and_gap(later, later_shifts[later])
                 if following is not None:
                     if o == AHEAD_AT[0]:
                         next_logp = logs.tile([P, SIDES, ROWS], F32, name="logp")
@@ -337,7 +377,8 @@ def tile_tropicalattention_pa_kernel(
             for rt in range(ROW_TILES):
                 b, t = divmod(rt, SEQ // P)
                 first_head = b * HEADS + f * HEADS_PER_BLOCK
-                nc.sync.dma_start(
+                queue = nc.scalar if following is None and rt % 2 == 1 else nc.sync
+                queue.dma_start(
                     out=outs[j][first_head : first_head + HEADS_PER_BLOCK, t * P : (t + 1) * P, :]
                     .rearrange("h l o -> l h o"),
                     in_=y[:, rt, :, :],

@@ -35,7 +35,7 @@ LATER_AT = (6, 12)
 PAIR_ON_VECTOR = tuple(range(8, 63, 9))
 VECTOR_AHEAD = 9
 SCALAR_AHEAD = 2
-REFILL_AT = 55
+REFILL_AT = (55, 58)
 
 FLOPS = 3 * (2 * ROWS * D_IN * FEATURES + 2 * ROWS * HEADS * DK * DK)
 
@@ -265,7 +265,7 @@ def tile_tropicalattention_pa_kernel(
                 out=lead[:], in0=logp[:, 1, :], in1=logp[:, 0, :], op=ALU.subtract
             )
 
-        def side1_into_psum(logp):
+        def side1_turned(logp):
             rows_first = pairs.tile([P, ROW_TILES, P], F32, name="rows_first")
             for bank in range(ROW_HALVES):
                 turned = psum_tr.tile([P, TILES_PER_BANK, P], F32, name="turned", tag="bank")
@@ -275,6 +275,9 @@ def tile_tropicalattention_pa_kernel(
                 nc.scalar.copy(
                     out=rows_first[:, bank * TILES_PER_BANK : (bank + 1) * TILES_PER_BANK, :], in_=turned[:]
                 )
+            return rows_first
+
+        def turned_back(rows_first):
             halves = []
             for bank in range(ROW_HALVES):
                 back = psum_keep.tile([P, TILES_PER_BANK, P], F32, name="back%d" % bank)
@@ -311,7 +314,7 @@ def tile_tropicalattention_pa_kernel(
         for s in range(SIDES):
             side_logs(blocks[0][0], blocks[0][1], logp, s)
         side_difference(logp, lead)
-        log1_psum = side1_into_psum(logp)
+        log1_psum = turned_back(side1_turned(logp))
         later_shifts = {}
         for later in range(1, n_proj):
             later_shifts[later] = shifts(later)
@@ -321,6 +324,7 @@ def tile_tropicalattention_pa_kernel(
             next_logp = None
             next_lead = None
             next_log1_psum = None
+            next_rows_first = None
             prepared = {}
             halfway = {}
             y = results.tile([P, ROW_TILES, HEADS_PER_BLOCK, DK], F32, name="y")
@@ -338,8 +342,10 @@ def tile_tropicalattention_pa_kernel(
                         side_logs(following[0], following[1], next_logp, 1)
                     elif o == AHEAD_AT[2]:
                         side_difference(next_logp, next_lead)
-                    elif o == REFILL_AT:
-                        next_log1_psum = side1_into_psum(next_logp)
+                    elif o == REFILL_AT[0]:
+                        next_rows_first = side1_turned(next_logp)
+                    elif o == REFILL_AT[1]:
+                        next_log1_psum = turned_back(next_rows_first)
                 if o in vector_at:
                     halfway[vector_at[o]] = better_less_other(j, f, vector_at[o], logp, log1_psum)
                 if o + SCALAR_AHEAD in PAIR_ON_VECTOR:

@@ -30,12 +30,14 @@ BLOCKS = HEADS // HEADS_PER_BLOCK
 CHUNKS = FEATURES // HALF // SIDES
 QUADRANTS = 4
 SPAN = 128.0
-AHEAD_AT = (16, 32, 48)
+AHEAD_AT = (16, 32)
 LATER_AT = (6, 12)
-PAIR_ON_VECTOR = tuple(range(8, 63, 9))
-VECTOR_AHEAD = 9
-SCALAR_AHEAD = 2
+PAIR_ON_VECTOR = (15, 16, 31, 32, 55, 58)
 REFILL_AT = (55, 58)
+HALVES_AT = {15: (-5, -2), 16: (1, 4), 31: (8, 12), 32: (17, 21), 55: (26, 31), 58: (36, 41)}
+WORK_AHEAD = 4
+LEAD_AT = (55, 58)
+SCALAR_BOTH = (5, 24, 44)
 
 FLOPS = 3 * (2 * ROWS * D_IN * FEATURES + 2 * ROWS * HEADS * DK * DK)
 
@@ -68,11 +70,12 @@ def tile_tropicalattention_pa_kernel(
         setup = ctx.enter_context(tc.tile_pool(name="setup", bufs=2))
         logs = ctx.enter_context(tc.tile_pool(name="logs", bufs=2))
         relus = ctx.enter_context(tc.tile_pool(name="relus", bufs=2))
-        cands = ctx.enter_context(tc.tile_pool(name="cands", bufs=4))
+        cands = ctx.enter_context(tc.tile_pool(name="cands", bufs=6))
         results = ctx.enter_context(tc.tile_pool(name="results", bufs=2))
         psum_tr = ctx.enter_context(tc.psum_pool(name="psum_tr", bufs=6))
         psum_keep = ctx.enter_context(tc.psum_pool(name="psum_keep", bufs=1))
         pairs = ctx.enter_context(tc.tile_pool(name="pairs", bufs=2))
+        halves_pool = ctx.enter_context(tc.tile_pool(name="halves_pool", bufs=3))
 
         ident = keep.tile([P, P], F32, name="ident")
         masks.make_identity(nc, ident[:])
@@ -260,9 +263,10 @@ def tile_tropicalattention_pa_kernel(
                 nc.scalar.activation(out=relu[:], in_=acc[:], func=ACT.Relu)
                 nc.scalar.activation(out=logp[:, s, rows], in_=relu[:], func=ACT.Ln, bias=1.0)
 
-        def side_difference(logp, lead):
+        def side_difference(logp, lead, piece):
+            rows = slice(piece * ROWS // len(LEAD_AT), (piece + 1) * ROWS // len(LEAD_AT))
             nc.gpsimd.tensor_tensor(
-                out=lead[:], in0=logp[:, 1, :], in1=logp[:, 0, :], op=ALU.subtract
+                out=lead[:, rows], in0=logp[:, 1, rows], in1=logp[:, 0, rows], op=ALU.subtract
             )
 
         def side1_turned(logp):
@@ -286,17 +290,14 @@ def tile_tropicalattention_pa_kernel(
                 halves.append(back)
             return halves
 
-        def better_less_other(j, f, o, logp, log1_psum):
-            less = pairs.tile([P, ROWS], F32, name="pair_less")
-            for bank in range(ROW_HALVES):
-                rows = slice(bank * N_MOVING, (bank + 1) * N_MOVING)
-                nc.vector.scalar_tensor_tensor(
-                    out=less[:, rows], in0=logp[:, 0, rows],
-                    scalar=gaps[j][:, f, o : o + 1],
-                    in1=log1_psum[bank][:].rearrange("p r c -> p (r c)"),
-                    op0=ALU.subtract, op1=ALU.max,
-                )
-            return less
+        def better_less_other(j, f, o, logp, log1_psum, less, bank):
+            rows = slice(bank * N_MOVING, (bank + 1) * N_MOVING)
+            nc.vector.scalar_tensor_tensor(
+                out=less[:, rows], in0=logp[:, 0, rows],
+                scalar=gaps[j][:, f, o : o + 1],
+                in1=log1_psum[bank][:].rearrange("p r c -> p (r c)"),
+                op0=ALU.subtract, op1=ALU.max,
+            )
 
         def add_other(j, f, o, less):
             better = pairs.tile([P, ROWS], F32, name="pair_better")
@@ -306,87 +307,128 @@ def tile_tropicalattention_pa_kernel(
             return better
 
         blocks = [(j, f) for j in range(n_proj) for f in range(BLOCKS)]
+        steps = [(block, o) for block in range(len(blocks)) for o in range(DK)]
         vector_at = {}
         for pair_step in PAIR_ON_VECTOR:
-            vector_at[max(0, pair_step - VECTOR_AHEAD)] = pair_step
-        logp = logs.tile([P, SIDES, ROWS], F32, name="logp")
-        lead = logs.tile([P, ROWS], F32, name="lead")
-        for s in range(SIDES):
-            side_logs(blocks[0][0], blocks[0][1], logp, s)
-        side_difference(logp, lead)
-        log1_psum = turned_back(side1_turned(logp))
-        later_shifts = {}
-        for later in range(1, n_proj):
-            later_shifts[later] = shifts(later)
+            for bank in range(ROW_HALVES):
+                vector_at[HALVES_AT[pair_step][bank]] = (pair_step, bank)
+        logps = {}
+        leads = {}
+        log1s = {}
+        rows_firsts = {}
+        halfway = {}
+        terms_of = {}
+        ys = {}
 
-        for index, (j, f) in enumerate(blocks):
-            following = blocks[index + 1] if index + 1 < len(blocks) else None
-            next_logp = None
-            next_lead = None
-            next_log1_psum = None
-            next_rows_first = None
-            prepared = {}
-            halfway = {}
-            y = results.tile([P, ROW_TILES, HEADS_PER_BLOCK, DK], F32, name="y")
-            for o in range(DK):
-                if index == 0 and o in LATER_AT:
-                    later = 1 + LATER_AT.index(o)
-                    scales_side_first(later)
-                    base_and_gap(later, later_shifts[later])
-                if following is not None:
-                    if o == AHEAD_AT[0]:
-                        next_logp = logs.tile([P, SIDES, ROWS], F32, name="logp")
-                        next_lead = logs.tile([P, ROWS], F32, name="lead")
-                        side_logs(following[0], following[1], next_logp, 0)
-                    elif o == AHEAD_AT[1]:
-                        side_logs(following[0], following[1], next_logp, 1)
-                    elif o == AHEAD_AT[2]:
-                        side_difference(next_logp, next_lead)
-                    elif o == REFILL_AT[0]:
-                        next_rows_first = side1_turned(next_logp)
-                    elif o == REFILL_AT[1]:
-                        next_log1_psum = turned_back(next_rows_first)
-                if o in vector_at:
-                    halfway[vector_at[o]] = better_less_other(j, f, vector_at[o], logp, log1_psum)
-                if o + SCALAR_AHEAD in PAIR_ON_VECTOR:
-                    prepared[o + SCALAR_AHEAD] = add_other(j, f, o + SCALAR_AHEAD, halfway[o + SCALAR_AHEAD])
-                if o in PAIR_ON_VECTOR:
-                    terms = [prepared[o][:]]
-                else:
-                    lower = cands.tile([P, ROWS], F32, name="lower")
-                    nc.gpsimd.tensor_scalar(
-                        out=lower[:], in0=logp[:, 0, :], scalar1=bases[j][:, f, o : o + 1],
-                        scalar2=1.0, op0=ALU.add, op1=ALU.mult,
-                    )
-                    excess = cands.tile([P, ROWS], F32, name="excess")
-                    nc.scalar.activation(
-                        out=excess[:], in_=lead[:], func=ACT.Relu, bias=gaps[j][:, f, o : o + 1]
-                    )
-                    terms = [lower[:], excess[:]]
-                for bank in range(ROW_TILES // TILES_PER_BANK):
-                    turned = psum_tr.tile([P, TILES_PER_BANK, P], F32, name="turned", tag="bank")
-                    for r in range(TILES_PER_BANK):
-                        rt = bank * TILES_PER_BANK + r
-                        for number, term in enumerate(terms):
-                            nc.tensor.matmul(
-                                out=turned[:, r, :], lhsT=term[:, rt * P : (rt + 1) * P],
-                                rhs=ident[:], is_transpose=True,
-                                start=(number == 0), stop=(number == len(terms) - 1),
-                            )
-                    nc.vector.tensor_reduce(
-                        out=y[:, bank * TILES_PER_BANK : (bank + 1) * TILES_PER_BANK, :, o],
-                        in_=turned[:].rearrange("p r (h i) -> p r h i", i=HALF),
-                        axis=mybir.AxisListType.X,
-                        op=ALU.max,
-                    )
+        def issue_half(block, at):
+            pair_step, bank = vector_at[at]
+            if bank == 0:
+                halfway[(block, pair_step)] = halves_pool.tile([P, ROWS], F32, name="pair_less")
+            better_less_other(
+                blocks[block][0], blocks[block][1], pair_step, logps[block], log1s[block],
+                halfway[(block, pair_step)], bank,
+            )
 
+        def produce(block, o):
+            j, f = blocks[block]
+            if o in PAIR_ON_VECTOR:
+                terms_of[(block, o)] = [add_other(j, f, o, halfway[(block, o)])[:]]
+                if o in LEAD_AT and block + 1 < len(blocks):
+                    side_difference(logps[block + 1], leads[block + 1], LEAD_AT.index(o))
+                return
+            lower = cands.tile([P, ROWS], F32, name="lower")
+            if o in SCALAR_BOTH:
+                nc.scalar.activation(
+                    out=lower[:], in_=logps[block][:, 0, :], func=ACT.Identity,
+                    bias=bases[j][:, f, o : o + 1],
+                )
+            else:
+                nc.gpsimd.tensor_scalar(
+                    out=lower[:], in0=logps[block][:, 0, :], scalar1=bases[j][:, f, o : o + 1],
+                    scalar2=1.0, op0=ALU.add, op1=ALU.mult,
+                )
+            excess = cands.tile([P, ROWS], F32, name="excess")
+            nc.scalar.activation(
+                out=excess[:], in_=leads[block][:], func=ACT.Relu, bias=gaps[j][:, f, o : o + 1]
+            )
+            terms_of[(block, o)] = [lower[:], excess[:]]
+
+        def beside(block, o):
+            following = block + 1
+            if following < len(blocks):
+                if o == AHEAD_AT[0]:
+                    logps[following] = logs.tile([P, SIDES, ROWS], F32, name="logp")
+                    leads[following] = logs.tile([P, ROWS], F32, name="lead")
+                if o in AHEAD_AT:
+                    side_logs(blocks[following][0], blocks[following][1], logps[following], AHEAD_AT.index(o))
+                if o == REFILL_AT[0]:
+                    rows_firsts[following] = side1_turned(logps[following])
+                elif o == REFILL_AT[1]:
+                    log1s[following] = turned_back(rows_firsts[following])
+                if o - DK in vector_at:
+                    issue_half(following, o - DK)
+            if o in vector_at:
+                issue_half(block, o)
+
+        def consume(block, o):
+            if o == 0:
+                ys[block] = results.tile([P, ROW_TILES, HEADS_PER_BLOCK, DK], F32, name="y")
+            terms = terms_of[(block, o)]
+            for bank in range(ROW_TILES // TILES_PER_BANK):
+                turned = psum_tr.tile([P, TILES_PER_BANK, P], F32, name="turned", tag="bank")
+                for r in range(TILES_PER_BANK):
+                    rt = bank * TILES_PER_BANK + r
+                    for number, term in enumerate(terms):
+                        nc.tensor.matmul(
+                            out=turned[:, r, :], lhsT=term[:, rt * P : (rt + 1) * P],
+                            rhs=ident[:], is_transpose=True,
+                            start=(number == 0), stop=(number == len(terms) - 1),
+                        )
+                nc.vector.tensor_reduce(
+                    out=ys[block][:, bank * TILES_PER_BANK : (bank + 1) * TILES_PER_BANK, :, o],
+                    in_=turned[:].rearrange("p r (h i) -> p r h i", i=HALF),
+                    axis=mybir.AxisListType.X,
+                    op=ALU.max,
+                )
+
+        def store(block):
+            j, f = blocks[block]
             for rt in range(ROW_TILES):
                 b, t = divmod(rt, SEQ // P)
                 first_head = b * HEADS + f * HEADS_PER_BLOCK
-                queue = nc.scalar if following is None and rt % 2 == 1 else nc.sync
+                queue = nc.scalar if block + 1 == len(blocks) and rt % 2 == 1 else nc.sync
                 queue.dma_start(
                     out=outs[j][first_head : first_head + HEADS_PER_BLOCK, t * P : (t + 1) * P, :]
                     .rearrange("h l o -> l h o"),
-                    in_=y[:, rt, :, :],
+                    in_=ys[block][:, rt, :, :],
                 )
-            logp, lead, log1_psum = next_logp, next_lead, next_log1_psum
+
+        ctx.enter_context(tc.manual_schedule())
+        logps[0] = logs.tile([P, SIDES, ROWS], F32, name="logp")
+        leads[0] = logs.tile([P, ROWS], F32, name="lead")
+        for s in range(SIDES):
+            side_logs(blocks[0][0], blocks[0][1], logps[0], s)
+        for piece in range(len(LEAD_AT)):
+            side_difference(logps[0], leads[0], piece)
+        log1s[0] = turned_back(side1_turned(logps[0]))
+        for number in range(WORK_AHEAD):
+            if steps[number][1] not in PAIR_ON_VECTOR:
+                produce(steps[number][0], steps[number][1])
+        later_shifts = {}
+        for later in range(1, n_proj):
+            later_shifts[later] = shifts(later)
+        for at in sorted(vector_at):
+            if at < 0:
+                issue_half(0, at)
+
+        for number, (block, o) in enumerate(steps):
+            if block == 0 and o in LATER_AT:
+                later = 1 + LATER_AT.index(o)
+                scales_side_first(later)
+                base_and_gap(later, later_shifts[later])
+            if number + WORK_AHEAD < len(steps):
+                produce(steps[number + WORK_AHEAD][0], steps[number + WORK_AHEAD][1])
+            beside(block, o)
+            consume(block, o)
+            if o == DK - 1:
+                store(block)

@@ -32,12 +32,14 @@ QUADRANTS = 4
 SPAN = 128.0
 AHEAD_AT = (16, 32)
 LATER_AT = (6, 12)
-PAIR_ON_VECTOR = (15, 16, 31, 32, 55, 58)
+PAIR_ON_VECTOR = (15, 16, 24, 31, 32, 44, 55, 58)
 REFILL_AT = (55, 58)
-HALVES_AT = {15: (-5, -2), 16: (1, 4), 31: (8, 12), 32: (17, 21), 55: (26, 31), 58: (36, 41)}
+HALVES_AT = {
+    15: (-5, -2), 16: (1, 4), 24: (7, 10), 31: (13, 16), 32: (19, 22), 44: (25, 29), 55: (33, 37), 58: (41, 45),
+}
 WORK_AHEAD = 4
 LEAD_AT = (55, 58)
-SCALAR_BOTH = (5, 24, 44)
+SCALAR_BOTH = (5,)
 
 FLOPS = 3 * (2 * ROWS * D_IN * FEATURES + 2 * ROWS * HEADS * DK * DK)
 

@@ -37,7 +37,7 @@ REFILL_AT = (55, 58)
 HALVES_AT = {
     15: (-5, -2), 16: (1, 4), 24: (7, 10), 31: (13, 16), 32: (19, 22), 44: (25, 29), 55: (33, 37), 58: (41, 45),
 }
-WORK_AHEAD = 4
+WORK_AHEAD = 5
 LEAD_AT = (55, 58)
 SCALAR_BOTH = (5,)
 
@@ -72,7 +72,7 @@ def tile_tropicalattention_pa_kernel(
         setup = ctx.enter_context(tc.tile_pool(name="setup", bufs=2))
         logs = ctx.enter_context(tc.tile_pool(name="logs", bufs=2))
         relus = ctx.enter_context(tc.tile_pool(name="relus", bufs=2))
-        cands = ctx.enter_context(tc.tile_pool(name="cands", bufs=6))
+        cands = ctx.enter_context(tc.tile_pool(name="cands", bufs=7))
         results = ctx.enter_context(tc.tile_pool(name="results", bufs=2))
         psum_tr = ctx.enter_context(tc.psum_pool(name="psum_tr", bufs=6))
         psum_keep = ctx.enter_context(tc.psum_pool(name="psum_keep", bufs=1))

@@ -22,6 +22,7 @@ PASSES = D_IN // K_PASS
 ROW_TILES = ROWS // P
 N_MOVING = 512
 ROW_HALVES = ROWS // N_MOVING
+TILES_PER_LOAD = 1
 TILES_PER_BANK = N_MOVING // P
 SIDES = 2
 HALF = DK // SIDES
@@ -37,6 +38,8 @@ REFILL_AT = (55, 58)
 HALVES_AT = {
     15: (-5, -2), 16: (1, 4), 24: (7, 10), 31: (13, 16), 32: (19, 22), 44: (25, 29), 55: (33, 37), 58: (41, 45),
 }
+FIRST_FILL_AT = (1, 3)
+FIRST_HALVES_AT = (4, 5, 6, 8)
 WORK_AHEAD = 5
 LEAD_AT = (55, 58)
 SCALAR_BOTH = (5,)
@@ -68,8 +71,9 @@ def tile_tropicalattention_pa_kernel(
     n_proj = len(outs)
 
     with ExitStack() as ctx:
+        ctx.enter_context(tc.manual_schedule())
         keep = ctx.enter_context(tc.tile_pool(name="keep", bufs=1))
-        setup = ctx.enter_context(tc.tile_pool(name="setup", bufs=2))
+        setup = ctx.enter_context(tc.tile_pool(name="setup", bufs=1))
         logs = ctx.enter_context(tc.tile_pool(name="logs", bufs=2))
         relus = ctx.enter_context(tc.tile_pool(name="relus", bufs=2))
         cands = ctx.enter_context(tc.tile_pool(name="cands", bufs=7))
@@ -82,15 +86,27 @@ def tile_tropicalattention_pa_kernel(
         ident = keep.tile([P, P], F32, name="ident")
         masks.make_identity(nc, ident[:])
 
-        x_rows = x.flatten_outer_dims()
+        x_rows = x.flatten_outer_dims().rearrange("(p r) d -> p r d", r=ROW_TILES)
         x_sb = keep.tile([P, ROW_TILES, D_IN], BF16, name="x_sb")
+        tiles_per_half = ROW_TILES // ROW_HALVES
 
-        def load_x(rt):
-            nc.sync.dma_start(out=x_sb[:, rt, :], in_=x_rows[rt * P : (rt + 1) * P, :])
+        def load_x(half):
+            for first in range(half * tiles_per_half, (half + 1) * tiles_per_half, TILES_PER_LOAD):
+                tiles = slice(first, first + TILES_PER_LOAD)
+                nc.sync.dma_start(out=x_sb[:, tiles, :], in_=x_rows[:, tiles, :])
 
         w_codes = keep.tile(
             [P, n_proj, PASSES, SIDES, FEATURES // SIDES], U32, name="w_codes", align_bytes=64
         )
+
+        w_first = keep.tile([P, PASSES, SIDES, P], U32, name="w_first", align_bytes=64)
+
+        def first_codes_side_first():
+            for g in range(PASSES):
+                nc.vector.tensor_copy(
+                    out=w_first[:, g, :, :].bitcast(I32).rearrange("p s (c i) -> p s c i", i=HALF),
+                    in_=first_codes[:, g, :].rearrange("p (c s i) -> p s c i", s=SIDES, i=HALF),
+                )
 
         def load_codes(j, first_head, last_head):
             for g in range(PASSES):
@@ -148,13 +164,18 @@ def tile_tropicalattention_pa_kernel(
             t_bf = keep.tile([DK, DK], BF16, name="t_bf%d" % j)
             nc.scalar.dma_start(out=t_bf[:], in_=tropical[j])
             t_bfs.append(t_bf)
-        tiles_per_half = ROW_TILES // ROW_HALVES
-        for rt in range(tiles_per_half):
-            load_x(rt)
+        table_load = setup.tile([P, 1], F32, name="table_load")
+        nc.scalar.activation(out=table_load[:], in_=ident[:, 0:1], func=ACT.Ln, bias=1.0)
+        load_x(0)
         load_scale_rows(0)
-        load_codes(0, 0, HEADS_PER_BLOCK)
-        for rt in range(tiles_per_half, ROW_TILES):
-            load_x(rt)
+        first_words = HEADS_PER_BLOCK * DK
+        first_codes = setup.tile([P, PASSES, first_words], I32, name="first_codes")
+        for g in range(PASSES):
+            nc.sync.dma_start(
+                out=first_codes[:, g, :],
+                in_=weights[0][0][g].rearrange("p n t -> p (n t)").bitcast(I32)[:, 0:first_words],
+            )
+        load_x(1)
         load_codes(0, HEADS_PER_BLOCK, HEADS)
         for j in range(1, n_proj):
             load_scale_rows(j)
@@ -163,7 +184,7 @@ def tile_tropicalattention_pa_kernel(
         x_grouped = keep.tile([P, PASSES, ROWS * PACK], BF16, name="x_grouped", align_bytes=64)
         x_codes = keep.tile([P, PASSES, ROWS], U32, name="x_codes", align_bytes=64)
         x_scales = keep.tile([P, PASSES, ROWS], U8, name="x_scales", align_bytes=64)
-        for half in range(ROW_HALVES):
+        def turn_x(half):
             for rt in range(half * tiles_per_half, (half + 1) * tiles_per_half):
                 x_words = x_sb[:, rt, :].bitcast(F32)
                 xt = psum_tr.tile([P, PASSES, 2, P], F32, name="xt", tag="bank")
@@ -174,12 +195,14 @@ def tile_tropicalattention_pa_kernel(
                             x_words[:, 256 * g + u : 256 * (g + 1) : 2],
                             ident[:],
                         )
-                nc.vector.tensor_copy(
+                nc.scalar.copy(
                     out=x_grouped[:, :, rt * P * PACK : (rt + 1) * P * PACK]
                     .bitcast(F32)
                     .rearrange("p g (r u) -> p g r u", u=2),
                     in_=xt[:].rearrange("p g u r -> p g r u"),
                 )
+
+        def quantise_x(half):
             rows = slice(half * N_MOVING, (half + 1) * N_MOVING)
             for g in range(PASSES):
                 nc.vector.quantize_mx(
@@ -187,47 +210,50 @@ def tile_tropicalattention_pa_kernel(
                     scales=x_scales[:, g, rows],
                     in_=x_grouped[:, g, half * N_MOVING * PACK : (half + 1) * N_MOVING * PACK],
                 )
-            if half == 0:
-                scales_side_first(0)
 
         lam_sq = setup.tile([P, P], F32, name="lam_sq")
         nc.vector.memset(lam_sq[:], 0.0)
-        nc.vector.tensor_copy(out=lam_sq[0 : SIDES * BLOCKS, :], in_=lam_bf[:])
-        lam_ps = psum_tr.tile([P, P], F32, name="lam_ps", tag="bank")
-        nc.tensor.transpose(lam_ps[:], lam_sq[:], ident[:])
+        t_sq = setup.tile([P, n_proj, SIDES, HEADS_PER_BLOCK, HALF], F32, name="t_sq")
+        nc.vector.memset(t_sq[:], 0.0)
         lam_t = keep.tile([P, SIDES, BLOCKS], F32, name="lam_t")
-        nc.vector.tensor_copy(
-            out=lam_t[:].rearrange("p s f -> p (s f)"), in_=lam_ps[:, 0 : SIDES * BLOCKS]
-        )
+
+        def repeat_constants():
+            nc.vector.tensor_copy(out=lam_sq[0 : SIDES * BLOCKS, :], in_=lam_bf[:])
+            for j in range(n_proj):
+                nc.vector.tensor_copy(
+                    out=t_sq[0:DK, j, :, :, :],
+                    in_=t_bfs[j][:]
+                    .rearrange("o (s i) -> o s i", i=HALF)
+                    .unsqueeze(2)
+                    .to_broadcast([DK, SIDES, HEADS_PER_BLOCK, HALF]),
+                )
+
+        def turn_lam():
+            lam_ps = psum_tr.tile([P, P], F32, name="lam_ps", tag="bank")
+            nc.tensor.transpose(lam_ps[:], lam_sq[:], ident[:])
+            nc.vector.tensor_copy(
+                out=lam_t[:].rearrange("p s f -> p (s f)"), in_=lam_ps[:, 0 : SIDES * BLOCKS]
+            )
+
+        bases, others, gaps, shift_of = {}, {}, {}, {}
 
         def shifts(j):
-            t_sq = setup.tile([P, SIDES, HEADS_PER_BLOCK, HALF], F32, name="t_sq")
-            nc.vector.memset(t_sq[:], 0.0)
             t_ps = psum_tr.tile([P, SIDES, P], F32, name="t_ps", tag="bank")
-            shift = setup.tile([P, SIDES, BLOCKS, DK], F32, name="shift")
             for s in range(SIDES):
-                nc.vector.tensor_copy(
-                    out=t_sq[0:DK, s, :, :],
-                    in_=t_bfs[j][:, s * HALF : (s + 1) * HALF]
-                    .unsqueeze(1)
-                    .to_broadcast([DK, HEADS_PER_BLOCK, HALF]),
-                )
                 nc.tensor.transpose(
-                    t_ps[:, s, :], t_sq[:, s, :, :].rearrange("p h i -> p (h i)"), ident[:]
+                    t_ps[:, s, :], t_sq[:, j, s, :, :].rearrange("p h i -> p (h i)"), ident[:]
                 )
-                nc.vector.tensor_tensor(
-                    out=shift[:, s, :, :],
-                    in0=t_ps[:, s, 0:DK].unsqueeze(1).to_broadcast([P, BLOCKS, DK]),
-                    in1=lam_t[:, s, :].unsqueeze(2).to_broadcast([P, BLOCKS, DK]),
-                    op=ALU.subtract,
-                )
-            return shift
+            shift = setup.tile([P, SIDES, BLOCKS, DK], F32, name="shift%d" % j)
+            nc.vector.tensor_tensor(
+                out=shift[:],
+                in0=t_ps[:, :, 0:DK].unsqueeze(2).to_broadcast([P, SIDES, BLOCKS, DK]),
+                in1=lam_t[:].unsqueeze(3).to_broadcast([P, SIDES, BLOCKS, DK]),
+                op=ALU.subtract,
+            )
+            shift_of[j] = shift
 
-        bases = {}
-        others = {}
-        gaps = {}
-
-        def base_and_gap(j, shift):
+        def base_and_gap(j):
+            shift = shift_of[j]
             base = keep.tile([P, BLOCKS, DK], F32, name="base%d" % j)
             nc.vector.scalar_tensor_tensor(
                 out=base[:], in0=shift[:, 1, :, :], scalar=-SPAN, in1=shift[:, 0, :, :],
@@ -244,32 +270,58 @@ def tile_tropicalattention_pa_kernel(
             others[j] = other
             gaps[j] = gap
 
-        base_and_gap(0, shifts(0))
+        blocks = [(j, f) for j in range(n_proj) for f in range(BLOCKS)]
+        steps = [(block, o) for block in range(len(blocks)) for o in range(DK)]
+        halves = [slice(half * N_MOVING, (half + 1) * N_MOVING) for half in range(ROW_HALVES)]
+        logps = {}
+        leads = {}
 
-        def side_logs(j, f, logp, s):
+        def side_logs(block, s, half):
+            j, f = blocks[block]
             cols = slice(f * P, (f + 1) * P)
-            for half in range(ROW_HALVES):
-                rows = slice(half * N_MOVING, (half + 1) * N_MOVING)
-                acc = psum_tr.tile([P, N_MOVING], F32, name="acc", tag="bank")
-                for g in range(PASSES):
-                    nc.tensor.matmul_mx(
-                        out=acc[:],
-                        lhsT=w_codes[:, j, g, s, cols].bitcast(FP8X4),
-                        lhsT_scale=w_scales[:, j, g, s, cols],
-                        rhs=x_codes[:, g, rows].bitcast(FP8X4),
-                        rhs_scale=x_scales[:, g, rows],
-                        start=(g == 0),
-                        stop=(g == PASSES - 1),
-                    )
-                relu = relus.tile([P, N_MOVING], F32, name="relu")
+            rows = halves[half]
+            acc = psum_tr.tile([P, N_MOVING], F32, name="acc", tag="bank")
+            for g in range(PASSES):
+                nc.tensor.matmul_mx(
+                    out=acc[:],
+                    lhsT=(w_first[:, g, s, :] if block == 0 else w_codes[:, j, g, s, cols]).bitcast(FP8X4),
+                    lhsT_scale=w_scales[:, j, g, s, cols],
+                    rhs=x_codes[:, g, rows].bitcast(FP8X4),
+                    rhs_scale=x_scales[:, g, rows],
+                    start=(g == 0),
+                    stop=(g == PASSES - 1),
+                )
+            relu = relus.tile([P, N_MOVING], F32, name="relu")
+            if block == 0:
+                nc.vector.tensor_scalar(out=relu[:], in0=acc[:], scalar1=0.0, scalar2=None, op0=ALU.max)
+            else:
                 nc.scalar.activation(out=relu[:], in_=acc[:], func=ACT.Relu)
-                nc.scalar.activation(out=logp[:, s, rows], in_=relu[:], func=ACT.Ln, bias=1.0)
+            nc.scalar.activation(out=logps[block][:, s, rows], in_=relu[:], func=ACT.Ln, bias=1.0)
 
-        def side_difference(logp, lead, piece):
-            rows = slice(piece * ROWS // len(LEAD_AT), (piece + 1) * ROWS // len(LEAD_AT))
-            nc.gpsimd.tensor_tensor(
-                out=lead[:, rows], in0=logp[:, 1, rows], in1=logp[:, 0, rows], op=ALU.subtract
+        def side_difference(engine, block, rows):
+            engine.tensor_tensor(
+                out=leads[block][:, rows], in0=logps[block][:, 1, rows], in1=logps[block][:, 0, rows],
+                op=ALU.subtract,
             )
+
+        logps[0] = logs.tile([P, SIDES, ROWS], F32, name="logp")
+        leads[0] = logs.tile([P, ROWS], F32, name="lead")
+        repeat_constants()
+        turn_x(0)
+        quantise_x(0)
+        scales_side_first(0)
+        first_codes_side_first()
+        turn_lam()
+        shifts(0)
+        turn_x(1)
+        for s in range(SIDES):
+            side_logs(0, s, 0)
+        quantise_x(1)
+        base_and_gap(0)
+        for s in range(SIDES):
+            side_logs(0, s, 1)
+        for rows in halves:
+            side_difference(nc.vector, 0, rows)
 
         def side1_turned(logp):
             rows_first = pairs.tile([P, ROW_TILES, P], F32, name="rows_first")
@@ -308,19 +360,17 @@ def tile_tropicalattention_pa_kernel(
             )
             return better
 
-        blocks = [(j, f) for j in range(n_proj) for f in range(BLOCKS)]
-        steps = [(block, o) for block in range(len(blocks)) for o in range(DK)]
         vector_at = {}
         for pair_step in PAIR_ON_VECTOR:
             for bank in range(ROW_HALVES):
                 vector_at[HALVES_AT[pair_step][bank]] = (pair_step, bank)
-        logps = {}
-        leads = {}
         log1s = {}
         rows_firsts = {}
         halfway = {}
         terms_of = {}
         ys = {}
+
+        early = sorted(vector_at)[: len(FIRST_HALVES_AT)]
 
         def issue_half(block, at):
             pair_step, bank = vector_at[at]
@@ -336,7 +386,7 @@ def tile_tropicalattention_pa_kernel(
             if o in PAIR_ON_VECTOR:
                 terms_of[(block, o)] = [add_other(j, f, o, halfway[(block, o)])[:]]
                 if o in LEAD_AT and block + 1 < len(blocks):
-                    side_difference(logps[block + 1], leads[block + 1], LEAD_AT.index(o))
+                    side_difference(nc.gpsimd, block + 1, halves[LEAD_AT.index(o)])
                 return
             lower = cands.tile([P, ROWS], F32, name="lower")
             if o in SCALAR_BOTH:
@@ -350,9 +400,15 @@ def tile_tropicalattention_pa_kernel(
                     scalar2=1.0, op0=ALU.add, op1=ALU.mult,
                 )
             excess = cands.tile([P, ROWS], F32, name="excess")
-            nc.scalar.activation(
-                out=excess[:], in_=leads[block][:], func=ACT.Relu, bias=gaps[j][:, f, o : o + 1]
-            )
+            if (block, o) == (0, 0):
+                nc.vector.tensor_scalar(
+                    out=excess[:], in0=leads[block][:], scalar1=gaps[j][:, f, o : o + 1], scalar2=0.0,
+                    op0=ALU.add, op1=ALU.max,
+                )
+            else:
+                nc.scalar.activation(
+                    out=excess[:], in_=leads[block][:], func=ACT.Relu, bias=gaps[j][:, f, o : o + 1]
+                )
             terms_of[(block, o)] = [lower[:], excess[:]]
 
         def beside(block, o):
@@ -362,19 +418,21 @@ def tile_tropicalattention_pa_kernel(
                     logps[following] = logs.tile([P, SIDES, ROWS], F32, name="logp")
                     leads[following] = logs.tile([P, ROWS], F32, name="lead")
                 if o in AHEAD_AT:
-                    side_logs(blocks[following][0], blocks[following][1], logps[following], AHEAD_AT.index(o))
+                    for half in range(ROW_HALVES):
+                        side_logs(following, AHEAD_AT.index(o), half)
                 if o == REFILL_AT[0]:
                     rows_firsts[following] = side1_turned(logps[following])
                 elif o == REFILL_AT[1]:
                     log1s[following] = turned_back(rows_firsts[following])
                 if o - DK in vector_at:
                     issue_half(following, o - DK)
-            if o in vector_at:
+            if o in vector_at and not (block == 0 and o in early):
                 issue_half(block, o)
+
 
         def consume(block, o):
             if o == 0:
-                ys[block] = results.tile([P, ROW_TILES, HEADS_PER_BLOCK, DK], F32, name="y")
+                ys[block] = results.tile([P, HEADS_PER_BLOCK, ROW_TILES, DK], F32, name="y")
             terms = terms_of[(block, o)]
             for bank in range(ROW_TILES // TILES_PER_BANK):
                 turned = psum_tr.tile([P, TILES_PER_BANK, P], F32, name="turned", tag="bank")
@@ -387,7 +445,8 @@ def tile_tropicalattention_pa_kernel(
                             start=(number == 0), stop=(number == len(terms) - 1),
                         )
                 nc.vector.tensor_reduce(
-                    out=ys[block][:, bank * TILES_PER_BANK : (bank + 1) * TILES_PER_BANK, :, o],
+                    out=ys[block][:, :, bank * TILES_PER_BANK : (bank + 1) * TILES_PER_BANK, o]
+                    .rearrange("p h r -> p r h"),
                     in_=turned[:].rearrange("p r (h i) -> p r h i", i=HALF),
                     axis=mybir.AxisListType.X,
                     op=ALU.max,
@@ -395,39 +454,32 @@ def tile_tropicalattention_pa_kernel(
 
         def store(block):
             j, f = blocks[block]
-            for rt in range(ROW_TILES):
-                b, t = divmod(rt, SEQ // P)
+            span = SEQ // ROW_TILES
+            for b in range(BATCH):
                 first_head = b * HEADS + f * HEADS_PER_BLOCK
-                queue = nc.scalar if block + 1 == len(blocks) and rt % 2 == 1 else nc.sync
+                queue = nc.scalar if block + 1 == len(blocks) and b % 2 == 1 else nc.sync
                 queue.dma_start(
-                    out=outs[j][first_head : first_head + HEADS_PER_BLOCK, t * P : (t + 1) * P, :]
-                    .rearrange("h l o -> l h o"),
-                    in_=ys[block][:, rt, :, :],
+                    out=outs[j][first_head : first_head + HEADS_PER_BLOCK, :, :]
+                    .rearrange("h (p r) o -> p h (r o)", r=ROW_TILES),
+                    in_=ys[block][b * span : (b + 1) * span, :, :, :].rearrange("p h r o -> p h (r o)"),
                 )
 
-        ctx.enter_context(tc.manual_schedule())
-        logps[0] = logs.tile([P, SIDES, ROWS], F32, name="logp")
-        leads[0] = logs.tile([P, ROWS], F32, name="lead")
-        for s in range(SIDES):
-            side_logs(blocks[0][0], blocks[0][1], logps[0], s)
-        for piece in range(len(LEAD_AT)):
-            side_difference(logps[0], leads[0], piece)
-        log1s[0] = turned_back(side1_turned(logps[0]))
         for number in range(WORK_AHEAD):
             if steps[number][1] not in PAIR_ON_VECTOR:
                 produce(steps[number][0], steps[number][1])
-        later_shifts = {}
-        for later in range(1, n_proj):
-            later_shifts[later] = shifts(later)
-        for at in sorted(vector_at):
-            if at < 0:
-                issue_half(0, at)
 
         for number, (block, o) in enumerate(steps):
             if block == 0 and o in LATER_AT:
                 later = 1 + LATER_AT.index(o)
                 scales_side_first(later)
-                base_and_gap(later, later_shifts[later])
+                shifts(later)
+                base_and_gap(later)
+            if number == FIRST_FILL_AT[0]:
+                rows_firsts[0] = side1_turned(logps[0])
+            elif number == FIRST_FILL_AT[1]:
+                log1s[0] = turned_back(rows_firsts[0])
+            if block == 0 and o in FIRST_HALVES_AT:
+                issue_half(0, early[FIRST_HALVES_AT.index(o)])
             if number + WORK_AHEAD < len(steps):
                 produce(steps[number + WORK_AHEAD][0], steps[number + WORK_AHEAD][1])
             beside(block, o)

@@ -44,6 +44,8 @@ WORK_AHEAD = 5
 LEAD_AT = (55, 58)
 SCALAR_BOTH = (5,)
 
+LINE = 512
+
 FLOPS = 3 * (2 * ROWS * D_IN * FEATURES + 2 * ROWS * HEADS * DK * DK)
 
 
@@ -83,7 +85,7 @@ def tile_tropicalattention_pa_kernel(
         pairs = ctx.enter_context(tc.tile_pool(name="pairs", bufs=2))
         halves_pool = ctx.enter_context(tc.tile_pool(name="halves_pool", bufs=3))
 
-        ident = keep.tile([P, P], F32, name="ident")
+        ident = keep.tile([P, P], F32, name="ident", align_bytes=LINE)
         masks.make_identity(nc, ident[:])
 
         x_rows = x.flatten_outer_dims().rearrange("(p r) d -> p r d", r=ROW_TILES)
@@ -291,7 +293,7 @@ def tile_tropicalattention_pa_kernel(
                     start=(g == 0),
                     stop=(g == PASSES - 1),
                 )
-            relu = relus.tile([P, N_MOVING], F32, name="relu")
+            relu = relus.tile([P, N_MOVING], F32, name="relu", align_bytes=LINE)
             if block == 0:
                 nc.vector.tensor_scalar(out=relu[:], in0=acc[:], scalar1=0.0, scalar2=None, op0=ALU.max)
             else:
@@ -304,8 +306,8 @@ def tile_tropicalattention_pa_kernel(
                 op=ALU.subtract,
             )
 
-        logps[0] = logs.tile([P, SIDES, ROWS], F32, name="logp")
-        leads[0] = logs.tile([P, ROWS], F32, name="lead")
+        logps[0] = logs.tile([P, SIDES, ROWS], F32, name="logp", align_bytes=LINE)
+        leads[0] = logs.tile([P, ROWS], F32, name="lead", align_bytes=LINE)
         repeat_constants()
         turn_x(0)
         quantise_x(0)
@@ -324,7 +326,7 @@ def tile_tropicalattention_pa_kernel(
             side_difference(nc.vector, 0, rows)
 
         def side1_turned(logp):
-            rows_first = pairs.tile([P, ROW_TILES, P], F32, name="rows_first")
+            rows_first = pairs.tile([P, ROW_TILES, P], F32, name="rows_first", align_bytes=LINE)
             for bank in range(ROW_HALVES):
                 turned = psum_tr.tile([P, TILES_PER_BANK, P], F32, name="turned", tag="bank")
                 for r in range(TILES_PER_BANK):
@@ -354,7 +356,7 @@ def tile_tropicalattention_pa_kernel(
             )
 
         def add_other(j, f, o, less):
-            better = pairs.tile([P, ROWS], F32, name="pair_better")
+            better = pairs.tile([P, ROWS], F32, name="pair_better", align_bytes=LINE)
             nc.scalar.activation(
                 out=better[:], in_=less[:], func=ACT.Identity, bias=others[j][:, f, o : o + 1]
             )
@@ -375,7 +377,7 @@ def tile_tropicalattention_pa_kernel(
         def issue_half(block, at):
             pair_step, bank = vector_at[at]
             if bank == 0:
-                halfway[(block, pair_step)] = halves_pool.tile([P, ROWS], F32, name="pair_less")
+                halfway[(block, pair_step)] = halves_pool.tile([P, ROWS], F32, name="pair_less", align_bytes=LINE)
             better_less_other(
                 blocks[block][0], blocks[block][1], pair_step, logps[block], log1s[block],
                 halfway[(block, pair_step)], bank,
@@ -388,7 +390,7 @@ def tile_tropicalattention_pa_kernel(
                 if o in LEAD_AT and block + 1 < len(blocks):
                     side_difference(nc.gpsimd, block + 1, halves[LEAD_AT.index(o)])
                 return
-            lower = cands.tile([P, ROWS], F32, name="lower")
+            lower = cands.tile([P, ROWS], F32, name="lower", align_bytes=LINE)
             if o in SCALAR_BOTH:
                 nc.scalar.activation(
                     out=lower[:], in_=logps[block][:, 0, :], func=ACT.Identity,
@@ -399,7 +401,7 @@ def tile_tropicalattention_pa_kernel(
                     out=lower[:], in0=logps[block][:, 0, :], scalar1=bases[j][:, f, o : o + 1],
                     scalar2=1.0, op0=ALU.add, op1=ALU.mult,
                 )
-            excess = cands.tile([P, ROWS], F32, name="excess")
+            excess = cands.tile([P, ROWS], F32, name="excess", align_bytes=LINE)
             if (block, o) == (0, 0):
                 nc.vector.tensor_scalar(
                     out=excess[:], in0=leads[block][:], scalar1=gaps[j][:, f, o : o + 1], scalar2=0.0,
@@ -415,8 +417,8 @@ def tile_tropicalattention_pa_kernel(
             following = block + 1
             if following < len(blocks):
                 if o == AHEAD_AT[0]:
-                    logps[following] = logs.tile([P, SIDES, ROWS], F32, name="logp")
-                    leads[following] = logs.tile([P, ROWS], F32, name="lead")
+                    logps[following] = logs.tile([P, SIDES, ROWS], F32, name="logp", align_bytes=LINE)
+                    leads[following] = logs.tile([P, ROWS], F32, name="lead", align_bytes=LINE)
                 if o in AHEAD_AT:
                     for half in range(ROW_HALVES):
                         side_logs(following, AHEAD_AT.index(o), half)
@@ -432,7 +434,7 @@ def tile_tropicalattention_pa_kernel(
 
         def consume(block, o):
             if o == 0:
-                ys[block] = results.tile([P, HEADS_PER_BLOCK, ROW_TILES, DK], F32, name="y")
+                ys[block] = results.tile([P, HEADS_PER_BLOCK, ROW_TILES, DK], F32, name="y", align_bytes=LINE)
             terms = terms_of[(block, o)]
             for bank in range(ROW_TILES // TILES_PER_BANK):
                 turned = psum_tr.tile([P, TILES_PER_BANK, P], F32, name="turned", tag="bank")

@@ -33,16 +33,15 @@ QUADRANTS = 4
 SPAN = 128.0
 AHEAD_AT = (16, 32)
 LATER_AT = (6, 12)
-PAIR_ON_VECTOR = (15, 16, 24, 31, 32, 44, 55, 58)
+PAIR_ON_VECTOR = (15, 16, 31, 32, 44, 55, 58)
 REFILL_AT = (55, 58)
 HALVES_AT = {
-    15: (-5, -2), 16: (1, 4), 24: (7, 10), 31: (13, 16), 32: (19, 22), 44: (25, 29), 55: (33, 37), 58: (41, 45),
+    15: (-5, -2), 16: (1, 4), 31: (8, 12), 32: (16, 20), 44: (24, 28), 55: (32, 37), 58: (42, 46),
 }
 FIRST_FILL_AT = (1, 3)
 FIRST_HALVES_AT = (4, 5, 6, 8)
 WORK_AHEAD = 5
 LEAD_AT = (55, 58)
-SCALAR_BOTH = (5,)
 
 LINE = 512
 
@@ -391,16 +390,10 @@ def tile_tropicalattention_pa_kernel(
                     side_difference(nc.gpsimd, block + 1, halves[LEAD_AT.index(o)])
                 return
             lower = cands.tile([P, ROWS], F32, name="lower", align_bytes=LINE)
-            if o in SCALAR_BOTH:
-                nc.scalar.activation(
-                    out=lower[:], in_=logps[block][:, 0, :], func=ACT.Identity,
-                    bias=bases[j][:, f, o : o + 1],
-                )
-            else:
-                nc.gpsimd.tensor_scalar(
-                    out=lower[:], in0=logps[block][:, 0, :], scalar1=bases[j][:, f, o : o + 1],
-                    scalar2=1.0, op0=ALU.add, op1=ALU.mult,
-                )
+            nc.gpsimd.tensor_scalar(
+                out=lower[:], in0=logps[block][:, 0, :], scalar1=bases[j][:, f, o : o + 1],
+                scalar2=1.0, op0=ALU.add, op1=ALU.mult,
+            )
             excess = cands.tile([P, ROWS], F32, name="excess", align_bytes=LINE)
             if (block, o) == (0, 0):
                 nc.vector.tensor_scalar(

from contextlib import ExitStack

import concourse.masks as masks
import concourse.mybir as mybir

F32 = mybir.dt.float32
BF16 = mybir.dt.bfloat16
I32 = mybir.dt.int32
U32 = mybir.dt.uint32
U8 = mybir.dt.uint8
FP8X4 = mybir.dt.float8_e4m3fn_x4
ACT = mybir.ActivationFunctionType
ALU = mybir.AluOpType

P = 128
BATCH, SEQ, D_IN, HEADS, DK = 4, 256, 1024, 16, 64
ROWS = BATCH * SEQ
FEATURES = HEADS * DK
PACK = 4
K_PASS = P * PACK
PASSES = D_IN // K_PASS
ROW_TILES = ROWS // P
N_MOVING = 512
ROW_HALVES = ROWS // N_MOVING
TILES_PER_LOAD = 1
TILES_PER_BANK = N_MOVING // P
SIDES = 2
HALF = DK // SIDES
HEADS_PER_BLOCK = P // HALF
BLOCKS = HEADS // HEADS_PER_BLOCK
CHUNKS = FEATURES // HALF // SIDES
QUADRANTS = 4
SPAN = 128.0
AHEAD_AT = (16, 32)
LATER_AT = (6, 12)
PAIR_ON_VECTOR = (15, 16, 31, 32, 44, 55, 58)
REFILL_AT = (55, 58)
HALVES_AT = {
    15: (-5, -2), 16: (1, 4), 31: (8, 12), 32: (16, 20), 44: (24, 28), 55: (32, 37), 58: (42, 46),
}
FIRST_FILL_AT = (1, 3)
FIRST_HALVES_AT = (4, 5, 6, 8)
WORK_AHEAD = 5
LEAD_AT = (55, 58)

LINE = 512

FLOPS = 3 * (2 * ROWS * D_IN * FEATURES + 2 * ROWS * HEADS * DK * DK)


def tile_tropicalattention_pa_kernel(
    tc,
    x,
    Wq_words,
    Wq_scales,
    Wk_words,
    Wk_scales,
    Wv_words,
    Wv_scales,
    lam,
    Wq_trop,
    Wk_trop,
    Wv_trop,
    out_0,
    out_1,
    out_2,
):
    nc = tc.nc
    weights = [(Wq_words, Wq_scales), (Wk_words, Wk_scales), (Wv_words, Wv_scales)]
    tropical = [Wq_trop, Wk_trop, Wv_trop]
    outs = [out_0, out_1, out_2]
    n_proj = len(outs)

    with ExitStack() as ctx:
        ctx.enter_context(tc.manual_schedule())
        keep = ctx.enter_context(tc.tile_pool(name="keep", bufs=1))
        setup = ctx.enter_context(tc.tile_pool(name="setup", bufs=1))
        logs = ctx.enter_context(tc.tile_pool(name="logs", bufs=2))
        relus = ctx.enter_context(tc.tile_pool(name="relus", bufs=2))
        cands = ctx.enter_context(tc.tile_pool(name="cands", bufs=7))
        results = ctx.enter_context(tc.tile_pool(name="results", bufs=2))
        psum_tr = ctx.enter_context(tc.psum_pool(name="psum_tr", bufs=6))
        psum_keep = ctx.enter_context(tc.psum_pool(name="psum_keep", bufs=1))
        pairs = ctx.enter_context(tc.tile_pool(name="pairs", bufs=2))
        halves_pool = ctx.enter_context(tc.tile_pool(name="halves_pool", bufs=3))

        ident = keep.tile([P, P], F32, name="ident", align_bytes=LINE)
        masks.make_identity(nc, ident[:])

        x_rows = x.flatten_outer_dims().rearrange("(p r) d -> p r d", r=ROW_TILES)
        x_sb = keep.tile([P, ROW_TILES, D_IN], BF16, name="x_sb")
        tiles_per_half = ROW_TILES // ROW_HALVES

        def load_x(half):
            for first in range(half * tiles_per_half, (half + 1) * tiles_per_half, TILES_PER_LOAD):
                tiles = slice(first, first + TILES_PER_LOAD)
                nc.sync.dma_start(out=x_sb[:, tiles, :], in_=x_rows[:, tiles, :])

        w_codes = keep.tile(
            [P, n_proj, PASSES, SIDES, FEATURES // SIDES], U32, name="w_codes", align_bytes=64
        )

        w_first = keep.tile([P, PASSES, SIDES, P], U32, name="w_first", align_bytes=64)

        def first_codes_side_first():
            for g in range(PASSES):
                nc.vector.tensor_copy(
                    out=w_first[:, g, :, :].bitcast(I32).rearrange("p s (c i) -> p s c i", i=HALF),
                    in_=first_codes[:, g, :].rearrange("p (c s i) -> p s c i", s=SIDES, i=HALF),
                )

        def load_codes(j, first_head, last_head):
            for g in range(PASSES):
                by_side = (
                    weights[j][0][g]
                    .rearrange("p n t -> p (n t)")
                    .bitcast(I32)
                    .rearrange("p (c s i) -> p c s i", s=SIDES, i=HALF)
                )
                for s in range(SIDES):
                    nc.sync.dma_start(
                        out=w_codes[:, j, g, s, first_head * HALF : last_head * HALF]
                        .bitcast(I32)
                        .rearrange("p (c i) -> p c i", i=HALF),
                        in_=by_side[:, first_head:last_head, s, :],
                    )

        raw_scales = keep.tile([P, n_proj, PASSES, FEATURES], U8, name="raw_scales")
        w_scales = keep.tile(
            [P, n_proj, PASSES, SIDES, FEATURES // SIDES], U8, name="w_scales", align_bytes=64
        )
        nc.vector.memset(raw_scales[:].bitcast(I32), 0)

        def load_scale_rows(j):
            scale_words = weights[j][1].bitcast(I32)
            for quad in range(QUADRANTS):
                nc.sync.dma_start(
                    out=raw_scales[32 * quad : 32 * quad + 4, j, :, :].bitcast(I32),
                    in_=scale_words[:, 4 * quad : 4 * quad + 4, :].rearrange("g q n -> q g n"),
                )

        def scales_side_first(j):
            raw_by_side = (
                raw_scales[:, j, :, :]
                .bitcast(I32)
                .rearrange("p g (c s w) -> p g c s w", s=SIDES, w=HALF // 4)
            )
            for s in range(SIDES):
                nc.vector.tensor_copy(
                    out=w_scales[:, j, :, s, :].bitcast(I32).rearrange("p g (c w) -> p g c w", w=HALF // 4),
                    in_=raw_by_side[:, :, :, s, :],
                )

        lam_bf = setup.tile([SIDES * BLOCKS, P], BF16, name="lam_bf")
        lam_by_side = lam.rearrange("a b n -> (a b) n").rearrange(
            "a (f h s i) -> a f h s i", h=HEADS_PER_BLOCK, s=SIDES, i=HALF
        )
        for s in range(SIDES):
            nc.scalar.dma_start(
                out=lam_bf[s * BLOCKS : (s + 1) * BLOCKS, :].rearrange("f (h i) -> f h i", i=HALF),
                in_=lam_by_side[0, :, :, s, :],
            )
        t_bfs = []
        for j in range(n_proj):
            t_bf = keep.tile([DK, DK], BF16, name="t_bf%d" % j)
            nc.scalar.dma_start(out=t_bf[:], in_=tropical[j])
            t_bfs.append(t_bf)
        table_load = setup.tile([P, 1], F32, name="table_load")
        nc.scalar.activation(out=table_load[:], in_=ident[:, 0:1], func=ACT.Ln, bias=1.0)
        load_x(0)
        load_scale_rows(0)
        first_words = HEADS_PER_BLOCK * DK
        first_codes = setup.tile([P, PASSES, first_words], I32, name="first_codes")
        for g in range(PASSES):
            nc.sync.dma_start(
                out=first_codes[:, g, :],
                in_=weights[0][0][g].rearrange("p n t -> p (n t)").bitcast(I32)[:, 0:first_words],
            )
        load_x(1)
        load_codes(0, HEADS_PER_BLOCK, HEADS)
        for j in range(1, n_proj):
            load_scale_rows(j)
            load_codes(j, 0, HEADS)

        x_grouped = keep.tile([P, PASSES, ROWS * PACK], BF16, name="x_grouped", align_bytes=64)
        x_codes = keep.tile([P, PASSES, ROWS], U32, name="x_codes", align_bytes=64)
        x_scales = keep.tile([P, PASSES, ROWS], U8, name="x_scales", align_bytes=64)
        def turn_x(half):
            for rt in range(half * tiles_per_half, (half + 1) * tiles_per_half):
                x_words = x_sb[:, rt, :].bitcast(F32)
                xt = psum_tr.tile([P, PASSES, 2, P], F32, name="xt", tag="bank")
                for g in range(PASSES):
                    for u in range(2):
                        nc.tensor.transpose(
                            xt[:, g, u, :],
                            x_words[:, 256 * g + u : 256 * (g + 1) : 2],
                            ident[:],
                        )
                nc.scalar.copy(
                    out=x_grouped[:, :, rt * P * PACK : (rt + 1) * P * PACK]
                    .bitcast(F32)
                    .rearrange("p g (r u) -> p g r u", u=2),
                    in_=xt[:].rearrange("p g u r -> p g r u"),
                )

        def quantise_x(half):
            rows = slice(half * N_MOVING, (half + 1) * N_MOVING)
            for g in range(PASSES):
                nc.vector.quantize_mx(
                    out=x_codes[:, g, rows].bitcast(FP8X4),
                    scales=x_scales[:, g, rows],
                    in_=x_grouped[:, g, half * N_MOVING * PACK : (half + 1) * N_MOVING * PACK],
                )

        lam_sq = setup.tile([P, P], F32, name="lam_sq")
        nc.vector.memset(lam_sq[:], 0.0)
        t_sq = setup.tile([P, n_proj, SIDES, HEADS_PER_BLOCK, HALF], F32, name="t_sq")
        nc.vector.memset(t_sq[:], 0.0)
        lam_t = keep.tile([P, SIDES, BLOCKS], F32, name="lam_t")

        def repeat_constants():
            nc.vector.tensor_copy(out=lam_sq[0 : SIDES * BLOCKS, :], in_=lam_bf[:])
            for j in range(n_proj):
                nc.vector.tensor_copy(
                    out=t_sq[0:DK, j, :, :, :],
                    in_=t_bfs[j][:]
                    .rearrange("o (s i) -> o s i", i=HALF)
                    .unsqueeze(2)
                    .to_broadcast([DK, SIDES, HEADS_PER_BLOCK, HALF]),
                )

        def turn_lam():
            lam_ps = psum_tr.tile([P, P], F32, name="lam_ps", tag="bank")
            nc.tensor.transpose(lam_ps[:], lam_sq[:], ident[:])
            nc.vector.tensor_copy(
                out=lam_t[:].rearrange("p s f -> p (s f)"), in_=lam_ps[:, 0 : SIDES * BLOCKS]
            )

        bases, others, gaps, shift_of = {}, {}, {}, {}

        def shifts(j):
            t_ps = psum_tr.tile([P, SIDES, P], F32, name="t_ps", tag="bank")
            for s in range(SIDES):
                nc.tensor.transpose(
                    t_ps[:, s, :], t_sq[:, j, s, :, :].rearrange("p h i -> p (h i)"), ident[:]
                )
            shift = setup.tile([P, SIDES, BLOCKS, DK], F32, name="shift%d" % j)
            nc.vector.tensor_tensor(
                out=shift[:],
                in0=t_ps[:, :, 0:DK].unsqueeze(2).to_broadcast([P, SIDES, BLOCKS, DK]),
                in1=lam_t[:].unsqueeze(3).to_broadcast([P, SIDES, BLOCKS, DK]),
                op=ALU.subtract,
            )
            shift_of[j] = shift

        def base_and_gap(j):
            shift = shift_of[j]
            base = keep.tile([P, BLOCKS, DK], F32, name="base%d" % j)
            nc.vector.scalar_tensor_tensor(
                out=base[:], in0=shift[:, 1, :, :], scalar=-SPAN, in1=shift[:, 0, :, :],
                op0=ALU.add, op1=ALU.max,
            )
            other = keep.tile([P, BLOCKS, DK], F32, name="other%d" % j)
            nc.vector.scalar_tensor_tensor(
                out=other[:], in0=shift[:, 0, :, :], scalar=-SPAN, in1=shift[:, 1, :, :],
                op0=ALU.add, op1=ALU.max,
            )
            gap = keep.tile([P, BLOCKS, DK], F32, name="gap%d" % j)
            nc.vector.tensor_tensor(out=gap[:], in0=other[:], in1=base[:], op=ALU.subtract)
            bases[j] = base
            others[j] = other
            gaps[j] = gap

        blocks = [(j, f) for j in range(n_proj) for f in range(BLOCKS)]
        steps = [(block, o) for block in range(len(blocks)) for o in range(DK)]
        halves = [slice(half * N_MOVING, (half + 1) * N_MOVING) for half in range(ROW_HALVES)]
        logps = {}
        leads = {}

        def side_logs(block, s, half):
            j, f = blocks[block]
            cols = slice(f * P, (f + 1) * P)
            rows = halves[half]
            acc = psum_tr.tile([P, N_MOVING], F32, name="acc", tag="bank")
            for g in range(PASSES):
                nc.tensor.matmul_mx(
                    out=acc[:],
                    lhsT=(w_first[:, g, s, :] if block == 0 else w_codes[:, j, g, s, cols]).bitcast(FP8X4),
                    lhsT_scale=w_scales[:, j, g, s, cols],
                    rhs=x_codes[:, g, rows].bitcast(FP8X4),
                    rhs_scale=x_scales[:, g, rows],
                    start=(g == 0),
                    stop=(g == PASSES - 1),
                )
            relu = relus.tile([P, N_MOVING], F32, name="relu", align_bytes=LINE)
            if block == 0:
                nc.vector.tensor_scalar(out=relu[:], in0=acc[:], scalar1=0.0, scalar2=None, op0=ALU.max)
            else:
                nc.scalar.activation(out=relu[:], in_=acc[:], func=ACT.Relu)
            nc.scalar.activation(out=logps[block][:, s, rows], in_=relu[:], func=ACT.Ln, bias=1.0)

        def side_difference(engine, block, rows):
            engine.tensor_tensor(
                out=leads[block][:, rows], in0=logps[block][:, 1, rows], in1=logps[block][:, 0, rows],
                op=ALU.subtract,
            )

        logps[0] = logs.tile([P, SIDES, ROWS], F32, name="logp", align_bytes=LINE)
        leads[0] = logs.tile([P, ROWS], F32, name="lead", align_bytes=LINE)
        repeat_constants()
        turn_x(0)
        quantise_x(0)
        scales_side_first(0)
        first_codes_side_first()
        turn_lam()
        shifts(0)
        turn_x(1)
        for s in range(SIDES):
            side_logs(0, s, 0)
        quantise_x(1)
        base_and_gap(0)
        for s in range(SIDES):
            side_logs(0, s, 1)
        for rows in halves:
            side_difference(nc.vector, 0, rows)

        def side1_turned(logp):
            rows_first = pairs.tile([P, ROW_TILES, P], F32, name="rows_first", align_bytes=LINE)
            for bank in range(ROW_HALVES):
                turned = psum_tr.tile([P, TILES_PER_BANK, P], F32, name="turned", tag="bank")
                for r in range(TILES_PER_BANK):
                    rt = bank * TILES_PER_BANK + r
                    nc.tensor.transpose(turned[:, r, :], logp[:, 1, rt * P : (rt + 1) * P], ident[:])
                nc.scalar.copy(
                    out=rows_first[:, bank * TILES_PER_BANK : (bank + 1) * TILES_PER_BANK, :], in_=turned[:]
                )
            return rows_first

        def turned_back(rows_first):
            halves = []
            for bank in range(ROW_HALVES):
                back = psum_keep.tile([P, TILES_PER_BANK, P], F32, name="back%d" % bank)
                for r in range(TILES_PER_BANK):
                    nc.tensor.transpose(back[:, r, :], rows_first[:, bank * TILES_PER_BANK + r, :], ident[:])
                halves.append(back)
            return halves

        def better_less_other(j, f, o, logp, log1_psum, less, bank):
            rows = slice(bank * N_MOVING, (bank + 1) * N_MOVING)
            nc.vector.scalar_tensor_tensor(
                out=less[:, rows], in0=logp[:, 0, rows],
                scalar=gaps[j][:, f, o : o + 1],
                in1=log1_psum[bank][:].rearrange("p r c -> p (r c)"),
                op0=ALU.subtract, op1=ALU.max,
            )

        def add_other(j, f, o, less):
            better = pairs.tile([P, ROWS], F32, name="pair_better", align_bytes=LINE)
            nc.scalar.activation(
                out=better[:], in_=less[:], func=ACT.Identity, bias=others[j][:, f, o : o + 1]
            )
            return better

        vector_at = {}
        for pair_step in PAIR_ON_VECTOR:
            for bank in range(ROW_HALVES):
                vector_at[HALVES_AT[pair_step][bank]] = (pair_step, bank)
        log1s = {}
        rows_firsts = {}
        halfway = {}
        terms_of = {}
        ys = {}

        early = sorted(vector_at)[: len(FIRST_HALVES_AT)]

        def issue_half(block, at):
            pair_step, bank = vector_at[at]
            if bank == 0:
                halfway[(block, pair_step)] = halves_pool.tile([P, ROWS], F32, name="pair_less", align_bytes=LINE)
            better_less_other(
                blocks[block][0], blocks[block][1], pair_step, logps[block], log1s[block],
                halfway[(block, pair_step)], bank,
            )

        def produce(block, o):
            j, f = blocks[block]
            if o in PAIR_ON_VECTOR:
                terms_of[(block, o)] = [add_other(j, f, o, halfway[(block, o)])[:]]
                if o in LEAD_AT and block + 1 < len(blocks):
                    side_difference(nc.gpsimd, block + 1, halves[LEAD_AT.index(o)])
                return
            lower = cands.tile([P, ROWS], F32, name="lower", align_bytes=LINE)
            nc.gpsimd.tensor_scalar(
                out=lower[:], in0=logps[block][:, 0, :], scalar1=bases[j][:, f, o : o + 1],
                scalar2=1.0, op0=ALU.add, op1=ALU.mult,
            )
            excess = cands.tile([P, ROWS], F32, name="excess", align_bytes=LINE)
            if (block, o) == (0, 0):
                nc.vector.tensor_scalar(
                    out=excess[:], in0=leads[block][:], scalar1=gaps[j][:, f, o : o + 1], scalar2=0.0,
                    op0=ALU.add, op1=ALU.max,
                )
            else:
                nc.scalar.activation(
                    out=excess[:], in_=leads[block][:], func=ACT.Relu, bias=gaps[j][:, f, o : o + 1]
                )
            terms_of[(block, o)] = [lower[:], excess[:]]

        def beside(block, o):
            following = block + 1
            if following < len(blocks):
                if o == AHEAD_AT[0]:
                    logps[following] = logs.tile([P, SIDES, ROWS], F32, name="logp", align_bytes=LINE)
                    leads[following] = logs.tile([P, ROWS], F32, name="lead", align_bytes=LINE)
                if o in AHEAD_AT:
                    for half in range(ROW_HALVES):
                        side_logs(following, AHEAD_AT.index(o), half)
                if o == REFILL_AT[0]:
                    rows_firsts[following] = side1_turned(logps[following])
                elif o == REFILL_AT[1]:
                    log1s[following] = turned_back(rows_firsts[following])
                if o - DK in vector_at:
                    issue_half(following, o - DK)
            if o in vector_at and not (block == 0 and o in early):
                issue_half(block, o)


        def consume(block, o):
            if o == 0:
                ys[block] = results.tile([P, HEADS_PER_BLOCK, ROW_TILES, DK], F32, name="y", align_bytes=LINE)
            terms = terms_of[(block, o)]
            for bank in range(ROW_TILES // TILES_PER_BANK):
                turned = psum_tr.tile([P, TILES_PER_BANK, P], F32, name="turned", tag="bank")
                for r in range(TILES_PER_BANK):
                    rt = bank * TILES_PER_BANK + r
                    for number, term in enumerate(terms):
                        nc.tensor.matmul(
                            out=turned[:, r, :], lhsT=term[:, rt * P : (rt + 1) * P],
                            rhs=ident[:], is_transpose=True,
                            start=(number == 0), stop=(number == len(terms) - 1),
                        )
                nc.vector.tensor_reduce(
                    out=ys[block][:, :, bank * TILES_PER_BANK : (bank + 1) * TILES_PER_BANK, o]
                    .rearrange("p h r -> p r h"),
                    in_=turned[:].rearrange("p r (h i) -> p r h i", i=HALF),
                    axis=mybir.AxisListType.X,
                    op=ALU.max,
                )

        def store(block):
            j, f = blocks[block]
            span = SEQ // ROW_TILES
            for b in range(BATCH):
                first_head = b * HEADS + f * HEADS_PER_BLOCK
                queue = nc.scalar if block + 1 == len(blocks) and b % 2 == 1 else nc.sync
                queue.dma_start(
                    out=outs[j][first_head : first_head + HEADS_PER_BLOCK, :, :]
                    .rearrange("h (p r) o -> p h (r o)", r=ROW_TILES),
                    in_=ys[block][b * span : (b + 1) * span, :, :, :].rearrange("p h r o -> p h (r o)"),
                )

        for number in range(WORK_AHEAD):
            if steps[number][1] not in PAIR_ON_VECTOR:
                produce(steps[number][0], steps[number][1])

        for number, (block, o) in enumerate(steps):
            if block == 0 and o in LATER_AT:
                later = 1 + LATER_AT.index(o)
                scales_side_first(later)
                shifts(later)
                base_and_gap(later)
            if number == FIRST_FILL_AT[0]:
                rows_firsts[0] = side1_turned(logps[0])
            elif number == FIRST_FILL_AT[1]:
                log1s[0] = turned_back(rows_firsts[0])
            if block == 0 and o in FIRST_HALVES_AT:
                issue_half(0, early[FIRST_HALVES_AT.index(o)])
            if number + WORK_AHEAD < len(steps):
                produce(steps[number + WORK_AHEAD][0], steps[number + WORK_AHEAD][1])
            beside(block, o)
            consume(block, o)
            if o == DK - 1:
                store(block)
